import numpy as np
import ml_dtypes


def mxq(x, axis, fmt="e4m3"):
    dtype, down = {"e4m3": (ml_dtypes.float8_e4m3fn, 7), "e5m2": (ml_dtypes.float8_e5m2, 14)}[fmt]
    v = np.moveaxis(np.asarray(x, np.float32).astype(ml_dtypes.bfloat16).astype(np.float64), axis, -1)
    blocks = v.reshape(v.shape[:-1] + (-1, 32))
    amax = np.abs(blocks).max(-1, keepdims=True)
    byte = np.maximum(np.where(amax > 0, np.frexp(amax)[1] - 1 + 127, 0) - down, 1)
    scale = np.exp2(byte - 127.0)
    codes = (blocks / scale).astype(np.float32).astype(dtype).astype(np.float64)
    return np.moveaxis((codes * scale).reshape(v.shape), -1, axis)


WIDE = False


def mx_kscale(k):
    if not WIDE:
        return np.ones(k)
    levels = np.array([10, -10, 5, -5, 0])
    if k % 512:
        return np.exp2(np.random.permutation(np.resize(levels, k // 32))).repeat(32)
    a = np.empty((k // 512, 16))
    for p in range(k // 512):
        a[p, :8] = np.random.permutation(np.resize(levels, 8))
        for g in range(8):
            far = levels[np.abs(levels - a[p, g]) >= 10]
            a[p, g + 8] = far[np.random.randint(len(far))]
    return np.exp2(a.ravel()).repeat(32)


BF16 = ml_dtypes.bfloat16


def bf(x):
    return np.asarray(x, np.float32).astype(BF16)


def f64(x):
    return np.asarray(x).astype(np.float64)


B, F_IN, HID, E, G, H = 4096, 64, 1024, 32, 4, 8
BN_EPS = 1e-5
L1_EPS = 1e-6 ** 2
SELU_ALPHA = 1.6732632423543772
SELU_SCALE = 1.0507009873554805


def selu(v):
    return SELU_SCALE * np.where(v > 0.0, v, SELU_ALPHA * (np.exp(np.minimum(v, 0.0)) - 1.0))


def setup_inputs():
    s = mx_kscale(HID)
    t = s / s.min()
    col_std = 0.5 + np.random.random(HID)
    col_mean = 0.5 * np.random.standard_normal(HID)
    return {"h2": bf(np.random.standard_normal((B, HID)) * col_std + col_mean),
            "gamma": bf((1.0 + 0.1 * np.random.standard_normal(HID)) * t),
            "beta": bf(0.1 * np.random.standard_normal(HID) * t),
            "Wh": bf(np.random.standard_normal((H, G, HID, E)) / np.sqrt(HID) / t[:, None]),
            "bh": bf(0.3 * np.random.standard_normal((H, G, E)))}


def reference(h2, gamma, beta, Wh, bh):
    h2 = f64(h2)
    mu = h2.mean(axis=0)
    var = h2.var(axis=0)
    e = selu((h2 - mu) / np.sqrt(var + BN_EPS) * f64(gamma) + f64(beta))
    p = (mxq(e, 1, "e4m3") @ mxq(f64(Wh), 2, "e4m3")).transpose(2, 0, 1, 3)
    d = selu(p + f64(bh))
    a = np.abs(d)
    l1 = np.maximum(a.sum(axis=-1, keepdims=True), L1_EPS)
    return np.sign(d) * (a / l1)

@@ -1,0 +1,254 @@
+import math
+
+import concourse.bass as bass
+import concourse.mybir as mybir
+import concourse.tile as tile
+from concourse.masks import make_identity
+
+F32 = mybir.dt.float32
+BF16 = mybir.dt.bfloat16
+U32 = mybir.dt.uint32
+U8 = mybir.dt.uint8
+FP8X4 = mybir.dt.float8_e4m3fn_x4
+ALU = mybir.AluOpType
+ACT = mybir.ActivationFunctionType
+AXIS = mybir.AxisListType
+
+P = 128
+ROWS = 4096
+HID = 1024
+OUTS = 1024
+HEAD = 32
+ROW_TILES = ROWS // P
+WORD_BLOCKS = HID // 2 // P
+PLANES = 2 * WORD_BLOCKS
+PASSES = HID // 512
+
+LOAD_TILES = 4
+LOAD_COLS = LOAD_TILES * P
+STAT_COLS = 256
+UNIT = 512
+
+BN_EPS = 1e-5
+L1_EPS = 1e-12
+SELU_ALPHA = 1.6732632423543772
+SELU_SCALE = 1.0507009873554805
+SA = SELU_SCALE * SELU_ALPHA
+
+FLOPS = 2 * ROWS * HID * OUTS
+
+
+def tile_basicemotionpredictions_pa_t_kernel(tc, h2, gamma, beta, Wh, bh, out):
+    nc = tc.nc
+    h2_v = h2.rearrange("(p n) f -> p n f", n=ROW_TILES)
+    out_v = out.rearrange("(p n) h g e -> p n (h g e)", n=ROW_TILES)
+    wh_v = Wh.rearrange("h g (c q t) e -> q (h g c) (t e)", c=PASSES, q=P, t=4)
+
+    with tc.tile_pool(name="keep", bufs=1) as keep, tc.tile_pool(name="stream", bufs=3) as stream, tc.tile_pool(
+        name="qin", bufs=2
+    ) as qin, tc.tile_pool(name="work", bufs=2) as work, tc.tile_pool(name="codes", bufs=3) as codes, tc.tile_pool(
+        name="post", bufs=2
+    ) as post, tc.tile_pool(name="small", bufs=3) as small, tc.psum_pool(name="psum_mm", bufs=4) as psum_mm, tc.psum_pool(
+        name="psum_tr", bufs=4
+    ) as psum_tr:
+        warm = keep.tile([P, 1], F32)
+        nc.vector.memset(warm[:], 1.0)
+        warm_out = keep.tile([P, 1], F32)
+        nc.scalar.activation(out=warm_out[:], in_=warm[:], func=ACT.Sqrt)
+        zero = keep.tile([P, 1], F32)
+        nc.vector.memset(zero[:], 0.0)
+        ln_sa = keep.tile([P, 1], F32)
+        nc.vector.tensor_scalar_add(out=ln_sa[:], in0=zero[:], scalar1=math.log(SA))
+
+        ident = keep.tile([P, P], F32)
+        make_identity(nc, ident[:])
+
+        gamma_sb = keep.tile([P, PASSES, 4], BF16)
+        beta_sb = keep.tile([P, PASSES, 4], BF16)
+        bh_sb = keep.tile([P, OUTS // P], BF16)
+        nc.scalar.dma_start(out=gamma_sb[:], in_=gamma.rearrange("(c q t) -> q c t", c=PASSES, q=P))
+        nc.scalar.dma_start(out=beta_sb[:], in_=beta.rearrange("(c q t) -> q c t", c=PASSES, q=P))
+        with nc.allow_non_contiguous_dma(reason="1,024 bias values, one output to a partition"):
+            nc.scalar.dma_start(out=bh_sb[:], in_=bh.rearrange("h g e -> (h g e)").rearrange("(ob o) -> o ob", o=P))
+
+        bias_rel = keep.tile([P, OUTS // P], F32)
+        bias_exp = keep.tile([P, OUTS // P], F32)
+        nc.vector.tensor_copy(out=bias_rel[:], in_=bh_sb[:])
+        nc.vector.tensor_scalar_add(out=bias_exp[:], in0=bias_rel[:], scalar1=math.log(SELU_ALPHA))
+
+        x_t = keep.tile([P, WORD_BLOCKS, ROWS], F32)
+        stats = keep.tile([P, WORD_BLOCKS, ROWS // STAT_COLS, 6], F32)
+        for ld in range(ROW_TILES // LOAD_TILES):
+            x_sb = stream.tile([P, LOAD_TILES, HID], BF16, tag="stream")
+            nc.sync.dma_start(out=x_sb[:], in_=h2_v[:, LOAD_TILES * ld : LOAD_TILES * (ld + 1), :])
+            for wb in range(WORD_BLOCKS):
+                xt_ps = psum_tr.tile([P, LOAD_COLS], F32, tag="tr")
+                for i in range(LOAD_TILES):
+                    nc.tensor.transpose(
+                        xt_ps[:, P * i : P * (i + 1)],
+                        x_sb[:, i, :].bitcast(F32)[:, 256 * (wb // 2) + wb % 2 : 256 * (wb // 2 + 1) : 2],
+                        ident[:],
+                    )
+                nc.scalar.copy(out=x_t[:, wb, LOAD_COLS * ld : LOAD_COLS * (ld + 1)], in_=xt_ps[:])
+                for s in range(LOAD_COLS // STAT_COLS):
+                    first = LOAD_COLS * ld + STAT_COLS * s
+                    nc.vector.bn_stats(
+                        out=stats[:, wb, first // STAT_COLS, :],
+                        in_=x_t[:, wb, first : first + STAT_COLS].bitcast(BF16),
+                    )
+
+        w_raws = []
+        for hf in range(2):
+            w_raw = stream.tile([P, 16, PLANES, HEAD], BF16, tag="stream")
+            nc.sync.dma_start(
+                out=w_raw[:].rearrange("q hg (c t) e -> q (hg c) (t e)", t=4),
+                in_=wh_v[:, 32 * hf : 32 * (hf + 1), :],
+            )
+            w_raws.append(w_raw)
+
+        mv = keep.tile([P, PLANES, 2], F32)
+        for wb in range(WORD_BLOCKS):
+            for e2 in range(2):
+                nc.vector.bn_aggr(out=mv[:, 2 * wb + e2, :], in_=stats[:, wb, :, 3 * e2 : 3 * e2 + 3])
+        var_eps = keep.tile([P, PLANES], F32)
+        std = keep.tile([P, PLANES], F32)
+        rstd = keep.tile([P, PLANES], F32)
+        a_lin = keep.tile([P, PLANES], F32)
+        a_neg = keep.tile([P, PLANES], F32)
+        b_neg = keep.tile([P, PLANES], F32)
+        a_rel = keep.tile([P, PLANES], F32)
+        b_rel = keep.tile([P, PLANES], F32)
+        nc.vector.tensor_scalar_add(out=var_eps[:], in0=mv[:, :, 1], scalar1=BN_EPS)
+        nc.scalar.activation(out=std[:], in_=var_eps[:], func=ACT.Sqrt)
+        nc.vector.reciprocal(out=rstd[:], in_=std[:])
+        nc.vector.tensor_tensor(out=a_lin[:], in0=gamma_sb[:].rearrange("q c t -> q (c t)"), in1=rstd[:], op=ALU.mult)
+        nc.vector.tensor_tensor(out=b_neg[:], in0=mv[:, :, 0], in1=a_lin[:], op=ALU.mult)
+        nc.vector.tensor_tensor(out=b_neg[:], in0=b_neg[:], in1=beta_sb[:].rearrange("q c t -> q (c t)"), op=ALU.subtract)
+        nc.vector.tensor_scalar_mul(out=a_neg[:], in0=a_lin[:], scalar1=-1.0)
+        nc.vector.tensor_scalar_mul(out=a_rel[:], in0=a_lin[:], scalar1=SELU_SCALE)
+        neg_e0 = keep.tile([P, 1], F32)
+        nc.scalar.activation(out=neg_e0[:], in_=zero[:], func=ACT.Exp, bias=ln_sa[:])
+        nc.vector.tensor_scalar_mul(out=neg_e0[:], in0=neg_e0[:], scalar1=-1.0)
+        nc.vector.tensor_scalar(
+            out=b_rel[:], in0=b_neg[:], scalar1=-SELU_SCALE, scalar2=neg_e0[:], op0=ALU.mult, op1=ALU.add
+        )
+
+        w_codes = keep.tile([P, 2, PASSES, 512], U32, align_bytes=64)
+        w_scales = keep.tile([P, 2, PASSES, 512], U8, align_bytes=64)
+        for hf in range(2):
+            for c in range(PASSES):
+                w_grouped = qin.tile([P, 512, 4], BF16, tag="grouped", align_bytes=64)
+                nc.vector.tensor_copy(
+                    out=w_grouped[:].rearrange("q (hg e) t -> q hg e t", e=HEAD),
+                    in_=w_raws[hf][:, :, 4 * c : 4 * (c + 1), :].rearrange("q hg t e -> q hg e t"),
+                )
+                nc.vector.quantize_mx(
+                    out=w_codes[:, hf, c, :].bitcast(FP8X4),
+                    scales=w_scales[:, hf, c, :],
+                    in_=w_grouped[:].rearrange("q o t -> q (o t)"),
+                )
+
+        def quantise_pass(u, c, e_codes, e_scales):
+            e_exp = work.tile([P, 4, UNIT], F32)
+            e_lin = work.tile([P, 4, UNIT], F32)
+            for t in range(4):
+                wb = 2 * c + t // 2
+                plane = 4 * c + t
+                x_plane = (
+                    x_t[:, wb, UNIT * u : UNIT * (u + 1)]
+                    .bitcast(BF16)
+                    .rearrange("q (j e2) -> q j e2", e2=2)[:, :, t % 2]
+                )
+                nc.scalar.activation(
+                    out=e_exp[:, t, :], in_=x_plane, func=ACT.Relu,
+                    scale=a_neg[:, plane : plane + 1], bias=b_neg[:, plane : plane + 1],
+                )
+                nc.gpsimd.tensor_scalar(
+                    out=e_lin[:, t, :], in0=x_plane,
+                    scalar1=a_rel[:, plane : plane + 1], scalar2=b_rel[:, plane : plane + 1],
+                    op0=ALU.mult, op1=ALU.add,
+                )
+            nc.scalar.activation(out=e_exp[:], in_=e_exp[:], func=ACT.Exp, scale=-1.0, bias=ln_sa[:])
+            e_grouped = qin.tile([P, UNIT, 4], BF16, tag="grouped", align_bytes=64)
+            nc.vector.scalar_tensor_tensor(
+                out=e_grouped[:],
+                in0=e_lin[:].rearrange("q t j -> q j t"),
+                scalar=neg_e0[:],
+                in1=e_exp[:].rearrange("q t j -> q j t"),
+                op0=ALU.max,
+                op1=ALU.add,
+            )
+            nc.vector.quantize_mx(
+                out=e_codes[:, c, :].bitcast(FP8X4),
+                scales=e_scales[:, c, :],
+                in_=e_grouped[:].rearrange("q j t -> q (j t)"),
+            )
+
+        def heads(u, hf, e_codes, e_scales):
+            z_exp = post.tile([P, 4, UNIT], F32, bufs=3)
+            z_rel = post.tile([P, 4, UNIT], F32)
+            for ob4 in range(4):
+                ob = 4 * hf + ob4
+                w_cols = slice(P * ob4, P * (ob4 + 1))
+                acc = psum_mm.tile([P, UNIT], F32)
+                for c in range(PASSES):
+                    nc.tensor.matmul_mx(
+                        out=acc[:],
+                        lhsT=w_codes[:, hf, c, w_cols].bitcast(FP8X4),
+                        lhsT_scale=w_scales[:, hf, c, w_cols],
+                        rhs=e_codes[:, c, :].bitcast(FP8X4),
+                        rhs_scale=e_scales[:, c, :],
+                        start=(c == 0),
+                        stop=(c == PASSES - 1),
+                    )
+                nc.scalar.activation(out=z_exp[:, ob4, :], in_=acc[:], func=ACT.Exp, bias=bias_exp[:, ob : ob + 1])
+                nc.scalar.activation(out=z_rel[:, ob4, :], in_=acc[:], func=ACT.Relu, bias=bias_rel[:, ob : ob + 1])
+            nc.vector.scalar_tensor_tensor(
+                out=z_exp[:], in0=z_exp[:], scalar=-SELU_ALPHA, in1=z_rel[:], op0=ALU.add, op1=ALU.min
+            )
+            l1 = small.tile([P, 4, 512 // HEAD], F32)
+            r_l1 = small.tile([P, 4, 512 // HEAD], F32)
+            d_abs = post.tile([P, 4, 512], F32)
+            d_ts = []
+            for nt in range(4):
+                d_t = psum_tr.tile([P, 512], F32, tag="tr")
+                for ob4 in range(4):
+                    nc.tensor.transpose(
+                        d_t[:, P * ob4 : P * (ob4 + 1)], z_exp[:, ob4, P * nt : P * (nt + 1)], ident[:]
+                    )
+                nc.scalar.activation(out=d_abs[:, nt, :], in_=d_t[:], func=ACT.Abs)
+                d_ts.append(d_t)
+            nc.vector.tensor_reduce(
+                out=l1[:].rearrange("p nt g -> p (nt g)"),
+                in_=d_abs[:].rearrange("p nt (g e) -> p (nt g) e", e=HEAD),
+                axis=AXIS.X,
+                op=ALU.add,
+            )
+            nc.vector.tensor_scalar_max(out=l1[:], in0=l1[:], scalar1=L1_EPS / SELU_SCALE)
+            nc.vector.reciprocal(out=r_l1[:], in_=l1[:])
+            out_sb = stream.tile([P, 4, 512], F32, tag="stream")
+            for nt in range(4):
+                nc.vector.tensor_tensor(
+                    out=out_sb[:, nt, :].rearrange("p (g e) -> p g e", e=HEAD),
+                    in0=d_ts[nt][:].rearrange("p (g e) -> p g e", e=HEAD),
+                    in1=r_l1[:, nt, :].unsqueeze(2).to_broadcast([P, 512 // HEAD, HEAD]),
+                    op=ALU.mult,
+                )
+            first_tile = UNIT * u // P
+            nc.sync.dma_start(out=out_v[:, first_tile : first_tile + 4, 512 * hf : 512 * (hf + 1)], in_=out_sb[:])
+
+        def quantise_unit(u):
+            e_codes = codes.tile([P, PASSES, UNIT], U32, align_bytes=64)
+            e_scales = codes.tile([P, PASSES, UNIT], U8, align_bytes=64)
+            for c in range(PASSES):
+                quantise_pass(u, c, e_codes, e_scales)
+            return e_codes, e_scales
+
+        units = ROWS // UNIT
+        ahead = quantise_unit(0)
+        for u in range(units):
+            now = ahead
+            if u + 1 < units:
+                ahead = quantise_unit(u + 1)
+            for hf in range(2):
+                heads(u, hf, now[0], now[1])

@@ -48,9 +48,9 @@ def tile_basicemotionpredictions_pa_t_kernel(tc, h2, gamma, beta, Wh, bh, out):
         name="qin", bufs=2
     ) as qin, tc.tile_pool(name="work", bufs=2) as work, tc.tile_pool(name="codes", bufs=3) as codes, tc.tile_pool(
         name="post", bufs=2
-    ) as post, tc.tile_pool(name="small", bufs=3) as small, tc.psum_pool(name="psum_mm", bufs=4) as psum_mm, tc.psum_pool(
+    ) as post, tc.tile_pool(name="small", bufs=3) as small, tc.psum_pool(name="psum_mm", bufs=3) as psum_mm, tc.psum_pool(
         name="psum_tr", bufs=4
-    ) as psum_tr:
+    ) as psum_tr, tc.psum_pool(name="psum_l1", bufs=1) as psum_l1:
         warm = keep.tile([P, 1], F32)
         nc.vector.memset(warm[:], 1.0)
         warm_out = keep.tile([P, 1], F32)
@@ -62,6 +62,10 @@ def tile_basicemotionpredictions_pa_t_kernel(tc, h2, gamma, beta, Wh, bh, out):
 
         ident = keep.tile([P, P], F32)
         make_identity(nc, ident[:])
+        heads_of = keep.tile([P, P // HEAD], F32)
+        nc.vector.memset(heads_of[:], 0.0)
+        for h in range(P // HEAD):
+            nc.vector.memset(heads_of[HEAD * h : HEAD * (h + 1), h : h + 1], 1.0)
 
         gamma_sb = keep.tile([P, PASSES, 4], BF16)
         beta_sb = keep.tile([P, PASSES, 4], BF16)
@@ -114,7 +118,6 @@ def tile_basicemotionpredictions_pa_t_kernel(tc, h2, gamma, beta, Wh, bh, out):
         std = keep.tile([P, PLANES], F32)
         rstd = keep.tile([P, PLANES], F32)
         a_lin = keep.tile([P, PLANES], F32)
-        a_neg = keep.tile([P, PLANES], F32)
         b_neg = keep.tile([P, PLANES], F32)
         a_rel = keep.tile([P, PLANES], F32)
         b_rel = keep.tile([P, PLANES], F32)
@@ -124,11 +127,14 @@ def tile_basicemotionpredictions_pa_t_kernel(tc, h2, gamma, beta, Wh, bh, out):
         nc.vector.tensor_tensor(out=a_lin[:], in0=gamma_sb[:].rearrange("q c t -> q (c t)"), in1=rstd[:], op=ALU.mult)
         nc.vector.tensor_tensor(out=b_neg[:], in0=mv[:, :, 0], in1=a_lin[:], op=ALU.mult)
         nc.vector.tensor_tensor(out=b_neg[:], in0=b_neg[:], in1=beta_sb[:].rearrange("q c t -> q (c t)"), op=ALU.subtract)
-        nc.vector.tensor_scalar_mul(out=a_neg[:], in0=a_lin[:], scalar1=-1.0)
         nc.vector.tensor_scalar_mul(out=a_rel[:], in0=a_lin[:], scalar1=SELU_SCALE)
         neg_e0 = keep.tile([P, 1], F32)
         nc.scalar.activation(out=neg_e0[:], in_=zero[:], func=ACT.Exp, bias=ln_sa[:])
         nc.vector.tensor_scalar_mul(out=neg_e0[:], in0=neg_e0[:], scalar1=-1.0)
+        exp_bias = keep.tile([P, 1], F32)
+        nc.vector.tensor_scalar(
+            out=exp_bias[:], in0=neg_e0[:], scalar1=-1.0 / SELU_SCALE, scalar2=math.log(SA), op0=ALU.mult, op1=ALU.add
+        )
         nc.vector.tensor_scalar(
             out=b_rel[:], in0=b_neg[:], scalar1=-SELU_SCALE, scalar2=neg_e0[:], op0=ALU.mult, op1=ALU.add
         )
@@ -148,107 +154,165 @@ def tile_basicemotionpredictions_pa_t_kernel(tc, h2, gamma, beta, Wh, bh, out):
                     in_=w_grouped[:].rearrange("q o t -> q (o t)"),
                 )
 
-        def quantise_pass(u, c, e_codes, e_scales):
-            e_exp = work.tile([P, 4, UNIT], F32)
+        e_lins, e_exps, e_groups, e_codes, e_scales = {}, {}, {}, {}, {}
+
+        def linear(p):
+            u, c = divmod(p, PASSES)
             e_lin = work.tile([P, 4, UNIT], F32)
+            e_exp = work.tile([P, 4, UNIT], F32)
             for t in range(4):
-                wb = 2 * c + t // 2
                 plane = 4 * c + t
                 x_plane = (
-                    x_t[:, wb, UNIT * u : UNIT * (u + 1)]
+                    x_t[:, 2 * c + t // 2, UNIT * u : UNIT * (u + 1)]
                     .bitcast(BF16)
                     .rearrange("q (j e2) -> q j e2", e2=2)[:, :, t % 2]
                 )
-                nc.scalar.activation(
-                    out=e_exp[:, t, :], in_=x_plane, func=ACT.Relu,
-                    scale=a_neg[:, plane : plane + 1], bias=b_neg[:, plane : plane + 1],
-                )
-                nc.gpsimd.tensor_scalar(
+                nc.vector.tensor_scalar(
                     out=e_lin[:, t, :], in0=x_plane,
                     scalar1=a_rel[:, plane : plane + 1], scalar2=b_rel[:, plane : plane + 1],
                     op0=ALU.mult, op1=ALU.add,
                 )
-            nc.scalar.activation(out=e_exp[:], in_=e_exp[:], func=ACT.Exp, scale=-1.0, bias=ln_sa[:])
-            e_grouped = qin.tile([P, UNIT, 4], BF16, tag="grouped", align_bytes=64)
+            nc.vector.tensor_scalar(out=e_exp[:], in0=e_lin[:], scalar1=neg_e0[:], scalar2=None, op0=ALU.min)
+            e_lins[p], e_exps[p] = e_lin, e_exp
+
+        def exponential(p):
+            nc.scalar.activation(out=e_exps[p][:], in_=e_exps[p][:], func=ACT.Exp, scale=1.0 / SELU_SCALE, bias=exp_bias[:])
+
+        def combine(p):
+            e_group = qin.tile([P, UNIT, 4], BF16, tag="grouped", align_bytes=64)
             nc.vector.scalar_tensor_tensor(
-                out=e_grouped[:],
-                in0=e_lin[:].rearrange("q t j -> q j t"),
+                out=e_group[:],
+                in0=e_lins[p][:].rearrange("q t j -> q j t"),
                 scalar=neg_e0[:],
-                in1=e_exp[:].rearrange("q t j -> q j t"),
+                in1=e_exps[p][:].rearrange("q t j -> q j t"),
                 op0=ALU.max,
                 op1=ALU.add,
             )
+            e_groups[p] = e_group
+
+        def quantise(p):
+            u, c = divmod(p, PASSES)
+            if c == 0:
+                codes_u = codes.tile([P, PASSES, UNIT], U32, align_bytes=64)
+                scales_u = codes.tile([P, PASSES, UNIT], U8, align_bytes=64)
+                e_codes[u], e_scales[u] = codes_u, scales_u
             nc.vector.quantize_mx(
-                out=e_codes[:, c, :].bitcast(FP8X4),
-                scales=e_scales[:, c, :],
-                in_=e_grouped[:].rearrange("q j t -> q (j t)"),
+                out=e_codes[u][:, c, :].bitcast(FP8X4),
+                scales=e_scales[u][:, c, :],
+                in_=e_groups[p][:].rearrange("q j t -> q (j t)"),
             )
 
-        def heads(u, hf, e_codes, e_scales):
-            z_exp = post.tile([P, 4, UNIT], F32, bufs=3)
-            z_rel = post.tile([P, 4, UNIT], F32)
-            for ob4 in range(4):
-                ob = 4 * hf + ob4
-                w_cols = slice(P * ob4, P * (ob4 + 1))
-                acc = psum_mm.tile([P, UNIT], F32)
-                for c in range(PASSES):
-                    nc.tensor.matmul_mx(
-                        out=acc[:],
-                        lhsT=w_codes[:, hf, c, w_cols].bitcast(FP8X4),
-                        lhsT_scale=w_scales[:, hf, c, w_cols],
-                        rhs=e_codes[:, c, :].bitcast(FP8X4),
-                        rhs_scale=e_scales[:, c, :],
-                        start=(c == 0),
-                        stop=(c == PASSES - 1),
-                    )
-                nc.scalar.activation(out=z_exp[:, ob4, :], in_=acc[:], func=ACT.Exp, bias=bias_exp[:, ob : ob + 1])
-                nc.scalar.activation(out=z_rel[:, ob4, :], in_=acc[:], func=ACT.Relu, bias=bias_rel[:, ob : ob + 1])
+        accs, z_exps, z_rels, d_abss, l1s, d_ts = {}, {}, {}, {}, {}, {}
+
+        def product(i, ob4):
+            u, hf = divmod(i, 2)
+            w_cols = slice(P * ob4, P * (ob4 + 1))
+            acc = psum_mm.tile([P, UNIT], F32)
+            for c in range(PASSES):
+                nc.tensor.matmul_mx(
+                    out=acc[:],
+                    lhsT=w_codes[:, hf, c, w_cols].bitcast(FP8X4),
+                    lhsT_scale=w_scales[:, hf, c, w_cols],
+                    rhs=e_codes[u][:, c, :].bitcast(FP8X4),
+                    rhs_scale=e_scales[u][:, c, :],
+                    start=(c == 0),
+                    stop=(c == PASSES - 1),
+                )
+            accs[i, ob4] = acc
+
+        def branches(i, ob4):
+            hf = i % 2
+            ob = 4 * hf + ob4
+            if ob4 == 0:
+                z_exp = post.tile([P, 4, UNIT], F32)
+                z_rel = post.tile([P, 4, UNIT], F32)
+                z_exps[i], z_rels[i] = z_exp, z_rel
+            acc = accs[i, ob4]
+            nc.scalar.activation(out=z_exps[i][:, ob4, :], in_=acc[:], func=ACT.Exp, bias=bias_exp[:, ob : ob + 1])
+            nc.scalar.activation(out=z_rels[i][:, ob4, :], in_=acc[:], func=ACT.Relu, bias=bias_rel[:, ob : ob + 1])
+
+        def head_selu(i):
             nc.vector.scalar_tensor_tensor(
-                out=z_exp[:], in0=z_exp[:], scalar=-SELU_ALPHA, in1=z_rel[:], op0=ALU.add, op1=ALU.min
+                out=z_exps[i][:], in0=z_exps[i][:], scalar=-SELU_ALPHA, in1=z_rels[i][:], op0=ALU.add, op1=ALU.min
             )
-            l1 = small.tile([P, 4, 512 // HEAD], F32)
-            r_l1 = small.tile([P, 4, 512 // HEAD], F32)
-            d_abs = post.tile([P, 4, 512], F32)
-            d_ts = []
+
+        def magnitudes(i):
+            nc.scalar.activation(out=z_rels[i][:], in_=z_exps[i][:], func=ACT.Abs)
+
+        def norms(i):
+            l1 = psum_l1.tile([P, 4, 512 // HEAD], F32)
+            for nt in range(4):
+                for ob4 in range(4):
+                    nc.tensor.matmul(
+                        l1[:, nt, 4 * ob4 : 4 * (ob4 + 1)],
+                        lhsT=z_rels[i][:, ob4, P * nt : P * (nt + 1)],
+                        rhs=heads_of[:],
+                        start=True,
+                        stop=True,
+                    )
+            l1s[i] = l1
+
+        def turn(i):
             for nt in range(4):
                 d_t = psum_tr.tile([P, 512], F32, tag="tr")
                 for ob4 in range(4):
                     nc.tensor.transpose(
-                        d_t[:, P * ob4 : P * (ob4 + 1)], z_exp[:, ob4, P * nt : P * (nt + 1)], ident[:]
+                        d_t[:, P * ob4 : P * (ob4 + 1)], z_exps[i][:, ob4, P * nt : P * (nt + 1)], ident[:]
                     )
-                nc.scalar.activation(out=d_abs[:, nt, :], in_=d_t[:], func=ACT.Abs)
-                d_ts.append(d_t)
-            nc.vector.tensor_reduce(
-                out=l1[:].rearrange("p nt g -> p (nt g)"),
-                in_=d_abs[:].rearrange("p nt (g e) -> p (nt g) e", e=HEAD),
-                axis=AXIS.X,
-                op=ALU.add,
-            )
-            nc.vector.tensor_scalar_max(out=l1[:], in0=l1[:], scalar1=L1_EPS / SELU_SCALE)
-            nc.vector.reciprocal(out=r_l1[:], in_=l1[:])
+                d_ts[i, nt] = d_t
+
+        def normalise(i):
+            u, hf = divmod(i, 2)
+            r_l1 = small.tile([P, 4, 512 // HEAD], F32)
+            nc.vector.tensor_scalar_max(out=r_l1[:], in0=l1s[i][:], scalar1=L1_EPS / SELU_SCALE)
+            nc.vector.reciprocal(out=r_l1[:], in_=r_l1[:])
             out_sb = stream.tile([P, 4, 512], F32, tag="stream")
             for nt in range(4):
                 nc.vector.tensor_tensor(
                     out=out_sb[:, nt, :].rearrange("p (g e) -> p g e", e=HEAD),
-                    in0=d_ts[nt][:].rearrange("p (g e) -> p g e", e=HEAD),
+                    in0=d_ts[i, nt][:].rearrange("p (g e) -> p g e", e=HEAD),
                     in1=r_l1[:, nt, :].unsqueeze(2).to_broadcast([P, 512 // HEAD, HEAD]),
                     op=ALU.mult,
                 )
             first_tile = UNIT * u // P
             nc.sync.dma_start(out=out_v[:, first_tile : first_tile + 4, 512 * hf : 512 * (hf + 1)], in_=out_sb[:])
 
-        def quantise_unit(u):
-            e_codes = codes.tile([P, PASSES, UNIT], U32, align_bytes=64)
-            e_scales = codes.tile([P, PASSES, UNIT], U8, align_bytes=64)
-            for c in range(PASSES):
-                quantise_pass(u, c, e_codes, e_scales)
-            return e_codes, e_scales
-
-        units = ROWS // UNIT
-        ahead = quantise_unit(0)
-        for u in range(units):
-            now = ahead
-            if u + 1 < units:
-                ahead = quantise_unit(u + 1)
-            for hf in range(2):
-                heads(u, hf, now[0], now[1])
+        steps = PASSES * ROWS // UNIT
+        with tc.manual_schedule():
+            linear(0)
+            exponential(0)
+            linear(1)
+            exponential(1)
+            combine(0)
+            combine(1)
+            quantise(0)
+            linear(2)
+            exponential(2)
+            quantise(1)
+            linear(3)
+            exponential(3)
+            combine(2)
+            for i in range(steps + 2):
+                if i < steps:
+                    for ob4 in range(3):
+                        product(i, ob4)
+                if i + 2 < steps:
+                    quantise(i + 2)
+                if 1 <= i <= steps:
+                    head_selu(i - 1)
+                    magnitudes(i - 1)
+                if i >= 2:
+                    normalise(i - 2)
+                if 1 <= i <= steps:
+                    norms(i - 1)
+                    turn(i - 1)
+                if i < steps:
+                    branches(i, 0)
+                    product(i, 3)
+                    for ob4 in range(1, 4):
+                        branches(i, ob4)
+                if i + 4 < steps:
+                    linear(i + 4)
+                    exponential(i + 4)
+                if i + 3 < steps:
+                    combine(i + 3)

@@ -19,6 +19,9 @@ ROWS = 4096
 HID = 1024
 OUTS = 1024
 HEAD = 32
+QUARTER = HEAD // 4
+HALF_HEADS = 16
+CLAMPED = 2
 ROW_TILES = ROWS // P
 WORD_BLOCKS = HID // 2 // P
 PLANES = 2 * WORD_BLOCKS
@@ -48,9 +51,9 @@ def tile_basicemotionpredictions_pa_t_kernel(tc, h2, gamma, beta, Wh, bh, out):
         name="qin", bufs=2
     ) as qin, tc.tile_pool(name="work", bufs=2) as work, tc.tile_pool(name="codes", bufs=3) as codes, tc.tile_pool(
         name="post", bufs=2
-    ) as post, tc.tile_pool(name="small", bufs=3) as small, tc.psum_pool(name="psum_mm", bufs=3) as psum_mm, tc.psum_pool(
-        name="psum_tr", bufs=4
-    ) as psum_tr, tc.psum_pool(name="psum_l1", bufs=1) as psum_l1:
+    ) as post, tc.tile_pool(name="small", bufs=3) as small, tc.psum_pool(name="psum_mm", bufs=4) as psum_mm, tc.psum_pool(
+        name="psum_tr", bufs=3
+    ) as psum_tr, tc.psum_pool(name="psum_abs", bufs=1) as psum_abs:
         warm = keep.tile([P, 1], F32)
         nc.vector.memset(warm[:], 1.0)
         warm_out = keep.tile([P, 1], F32)
@@ -62,23 +65,31 @@ def tile_basicemotionpredictions_pa_t_kernel(tc, h2, gamma, beta, Wh, bh, out):
 
         ident = keep.tile([P, P], F32)
         make_identity(nc, ident[:])
-        heads_of = keep.tile([P, P // HEAD], F32)
-        nc.vector.memset(heads_of[:], 0.0)
-        for h in range(P // HEAD):
-            nc.vector.memset(heads_of[HEAD * h : HEAD * (h + 1), h : h + 1], 1.0)
 
         gamma_sb = keep.tile([P, PASSES, 4], BF16)
         beta_sb = keep.tile([P, PASSES, 4], BF16)
-        bh_sb = keep.tile([P, OUTS // P], BF16)
+        bh_rows = keep.tile([P, P], BF16)
+        nc.vector.memset(bh_rows[:], 0.0)
+        bh_v = bh.rearrange("(hf a) g (k o) -> hf k (a g) o", hf=2, k=4)
+        for hf in range(2):
+            nc.scalar.dma_start(
+                out=bh_rows[4 * hf : 4 * (hf + 1), :].rearrange("k (h o) -> k h o", o=QUARTER), in_=bh_v[hf]
+            )
         nc.scalar.dma_start(out=gamma_sb[:], in_=gamma.rearrange("(c q t) -> q c t", c=PASSES, q=P))
         nc.scalar.dma_start(out=beta_sb[:], in_=beta.rearrange("(c q t) -> q c t", c=PASSES, q=P))
-        with nc.allow_non_contiguous_dma(reason="1,024 bias values, one output to a partition"):
-            nc.scalar.dma_start(out=bh_sb[:], in_=bh.rearrange("h g e -> (h g e)").rearrange("(ob o) -> o ob", o=P))
 
-        bias_rel = keep.tile([P, OUTS // P], F32)
+        bh_f32 = keep.tile([P, P], F32)
+        nc.vector.tensor_copy(out=bh_f32[:], in_=bh_rows[:])
+        bh_ps = psum_abs.tile([P, 512], F32, tag="abs")
+        nc.tensor.transpose(bh_ps[:, 0:P], bh_f32[:], ident[:])
+        bias = keep.tile([P, OUTS // P], F32)
         bias_exp = keep.tile([P, OUTS // P], F32)
-        nc.vector.tensor_copy(out=bias_rel[:], in_=bh_sb[:])
-        nc.vector.tensor_scalar_add(out=bias_exp[:], in0=bias_rel[:], scalar1=math.log(SELU_ALPHA))
+        neg_bias = keep.tile([P, OUTS // P], F32)
+        bias_minus = keep.tile([P, OUTS // P], F32)
+        nc.vector.tensor_copy(out=bias[:], in_=bh_ps[:, 0 : OUTS // P])
+        nc.vector.tensor_scalar_add(out=bias_exp[:], in0=bias[:], scalar1=math.log(SELU_ALPHA))
+        nc.vector.tensor_scalar_mul(out=neg_bias[:], in0=bias[:], scalar1=-1.0)
+        nc.vector.tensor_scalar_add(out=bias_minus[:], in0=bias[:], scalar1=-SELU_ALPHA)
 
         x_t = keep.tile([P, WORD_BLOCKS, ROWS], F32)
         stats = keep.tile([P, WORD_BLOCKS, ROWS // STAT_COLS, 6], F32)
@@ -144,10 +155,13 @@ def tile_basicemotionpredictions_pa_t_kernel(tc, h2, gamma, beta, Wh, bh, out):
         for hf in range(2):
             for c in range(PASSES):
                 w_grouped = qin.tile([P, 512, 4], BF16, tag="grouped", align_bytes=64)
-                nc.vector.tensor_copy(
-                    out=w_grouped[:].rearrange("q (hg e) t -> q hg e t", e=HEAD),
-                    in_=w_raws[hf][:, :, 4 * c : 4 * (c + 1), :].rearrange("q hg t e -> q hg e t"),
-                )
+                for k in range(4):
+                    nc.scalar.copy(
+                        out=w_grouped[:, P * k : P * (k + 1), :].rearrange("q (h o) t -> q h o t", o=QUARTER),
+                        in_=w_raws[hf][:, :, 4 * c : 4 * (c + 1), QUARTER * k : QUARTER * (k + 1)].rearrange(
+                            "q h t o -> q h o t"
+                        ),
+                    )
                 nc.vector.quantize_mx(
                     out=w_codes[:, hf, c, :].bitcast(FP8X4),
                     scales=w_scales[:, hf, c, :],
@@ -156,24 +170,25 @@ def tile_basicemotionpredictions_pa_t_kernel(tc, h2, gamma, beta, Wh, bh, out):
 
         e_lins, e_exps, e_groups, e_codes, e_scales = {}, {}, {}, {}, {}
 
-        def linear(p):
+        def x_plane(p, t):
             u, c = divmod(p, PASSES)
+            words = x_t[:, 2 * c + t // 2, UNIT * u : UNIT * (u + 1)]
+            return words.bitcast(BF16).rearrange("q (j e2) -> q j e2", e2=2)[:, :, t % 2]
+
+        def linear(p):
             e_lin = work.tile([P, 4, UNIT], F32)
-            e_exp = work.tile([P, 4, UNIT], F32)
             for t in range(4):
-                plane = 4 * c + t
-                x_plane = (
-                    x_t[:, 2 * c + t // 2, UNIT * u : UNIT * (u + 1)]
-                    .bitcast(BF16)
-                    .rearrange("q (j e2) -> q j e2", e2=2)[:, :, t % 2]
+                plane = 4 * (p % PASSES) + t
+                nc.scalar.activation(
+                    out=e_lin[:, t, :], in_=x_plane(p, t), func=ACT.Identity,
+                    scale=a_rel[:, plane : plane + 1], bias=b_rel[:, plane : plane + 1],
                 )
-                nc.vector.tensor_scalar(
-                    out=e_lin[:, t, :], in0=x_plane,
-                    scalar1=a_rel[:, plane : plane + 1], scalar2=b_rel[:, plane : plane + 1],
-                    op0=ALU.mult, op1=ALU.add,
-                )
-            nc.vector.tensor_scalar(out=e_exp[:], in0=e_lin[:], scalar1=neg_e0[:], scalar2=None, op0=ALU.min)
-            e_lins[p], e_exps[p] = e_lin, e_exp
+            e_lins[p] = e_lin
+
+        def clamp(p):
+            e_exp = work.tile([P, 4, UNIT], F32)
+            nc.vector.tensor_scalar(out=e_exp[:], in0=e_lins[p][:], scalar1=neg_e0[:], scalar2=None, op0=ALU.min)
+            e_exps[p] = e_exp
 
         def exponential(p):
             nc.scalar.activation(out=e_exps[p][:], in_=e_exps[p][:], func=ACT.Exp, scale=1.0 / SELU_SCALE, bias=exp_bias[:])
@@ -202,11 +217,11 @@ def tile_basicemotionpredictions_pa_t_kernel(tc, h2, gamma, beta, Wh, bh, out):
                 in_=e_groups[p][:].rearrange("q j t -> q (j t)"),
             )
 
-        accs, z_exps, z_rels, d_abss, l1s, d_ts = {}, {}, {}, {}, {}, {}
+        accs, ds, z_rels, d_abss, sums, d_ts, r_l1s, outs = {}, {}, {}, {}, {}, {}, {}, {}
 
-        def product(i, ob4):
+        def product(i, k):
             u, hf = divmod(i, 2)
-            w_cols = slice(P * ob4, P * (ob4 + 1))
+            w_cols = slice(P * k, P * (k + 1))
             acc = psum_mm.tile([P, UNIT], F32)
             for c in range(PASSES):
                 nc.tensor.matmul_mx(
@@ -218,101 +233,153 @@ def tile_basicemotionpredictions_pa_t_kernel(tc, h2, gamma, beta, Wh, bh, out):
                     start=(c == 0),
                     stop=(c == PASSES - 1),
                 )
-            accs[i, ob4] = acc
+            accs[i, k] = acc
 
-        def branches(i, ob4):
-            hf = i % 2
-            ob = 4 * hf + ob4
-            if ob4 == 0:
-                z_exp = post.tile([P, 4, UNIT], F32)
-                z_rel = post.tile([P, 4, UNIT], F32)
-                z_exps[i], z_rels[i] = z_exp, z_rel
-            acc = accs[i, ob4]
-            nc.scalar.activation(out=z_exps[i][:, ob4, :], in_=acc[:], func=ACT.Exp, bias=bias_exp[:, ob : ob + 1])
-            nc.scalar.activation(out=z_rels[i][:, ob4, :], in_=acc[:], func=ACT.Relu, bias=bias_rel[:, ob : ob + 1])
+        def branches(i):
+            d = post.tile([P, 4, UNIT], F32)
+            z_rel = post.tile([P, 4 - CLAMPED, UNIT], F32)
+            for k in range(4):
+                ob = 4 * (i % 2) + k
+                nc.scalar.activation(out=d[:, k, :], in_=accs[i, k][:], func=ACT.Exp, bias=bias_exp[:, ob : ob + 1])
+                if k >= CLAMPED:
+                    nc.scalar.activation(
+                        out=z_rel[:, k - CLAMPED, :], in_=accs[i, k][:], func=ACT.Relu, bias=bias[:, ob : ob + 1]
+                    )
+            ds[i], z_rels[i] = d, z_rel
 
-        def head_selu(i):
+        def head_clamp(i, k):
+            ob = 4 * (i % 2) + k
+            nc.vector.tensor_scalar(
+                out=ds[i][:, k, :], in0=ds[i][:, k, :],
+                scalar1=SELU_ALPHA, scalar2=bias_minus[:, ob : ob + 1], op0=ALU.min, op1=ALU.add,
+            )
+
+        def head_selu(i, k):
+            ob = 4 * (i % 2) + k
             nc.vector.scalar_tensor_tensor(
-                out=z_exps[i][:], in0=z_exps[i][:], scalar=-SELU_ALPHA, in1=z_rels[i][:], op0=ALU.add, op1=ALU.min
+                out=ds[i][:, k, :], in0=accs[i, k][:], scalar=neg_bias[:, ob : ob + 1], in1=ds[i][:, k, :],
+                op0=ALU.max, op1=ALU.add,
+            )
+
+        def head_selus(i):
+            for k in range(CLAMPED):
+                head_clamp(i, k)
+            for k in range(CLAMPED):
+                head_selu(i, k)
+            nc.vector.scalar_tensor_tensor(
+                out=ds[i][:, CLAMPED:, :], in0=ds[i][:, CLAMPED:, :], scalar=-SELU_ALPHA, in1=z_rels[i][:],
+                op0=ALU.add, op1=ALU.min,
             )
 
         def magnitudes(i):
-            nc.scalar.activation(out=z_rels[i][:], in_=z_exps[i][:], func=ACT.Abs)
+            d_abs = post.tile([P, 4, UNIT], F32)
+            nc.scalar.activation(out=d_abs[:], in_=ds[i][:], func=ACT.Abs)
+            d_abss[i] = d_abs
+
+        def turn(i, nt):
+            d_t = psum_tr.tile([P, 512], F32, tag="tr")
+            for k in range(4):
+                nc.tensor.transpose(d_t[:, P * k : P * (k + 1)], ds[i][:, k, P * nt : P * (nt + 1)], ident[:])
+            d_ts[i, nt] = d_t
+
+        def turn_magnitudes(i):
+            total = psum_abs.tile([P, 512], F32, tag="abs")
+            for nt in range(4):
+                for k in range(4):
+                    nc.tensor.matmul(
+                        total[:, P * nt : P * (nt + 1)],
+                        lhsT=d_abss[i][:, k, P * nt : P * (nt + 1)],
+                        rhs=ident[:],
+                        start=(k == 0),
+                        stop=(k == 3),
+                        is_transpose=True,
+                    )
+            sums[i] = total
 
         def norms(i):
-            l1 = psum_l1.tile([P, 4, 512 // HEAD], F32)
-            for nt in range(4):
-                for ob4 in range(4):
-                    nc.tensor.matmul(
-                        l1[:, nt, 4 * ob4 : 4 * (ob4 + 1)],
-                        lhsT=z_rels[i][:, ob4, P * nt : P * (nt + 1)],
-                        rhs=heads_of[:],
-                        start=True,
-                        stop=True,
-                    )
-            l1s[i] = l1
-
-        def turn(i):
-            for nt in range(4):
-                d_t = psum_tr.tile([P, 512], F32, tag="tr")
-                for ob4 in range(4):
-                    nc.tensor.transpose(
-                        d_t[:, P * ob4 : P * (ob4 + 1)], z_exps[i][:, ob4, P * nt : P * (nt + 1)], ident[:]
-                    )
-                d_ts[i, nt] = d_t
-
-        def normalise(i):
-            u, hf = divmod(i, 2)
-            r_l1 = small.tile([P, 4, 512 // HEAD], F32)
-            nc.vector.tensor_scalar_max(out=r_l1[:], in0=l1s[i][:], scalar1=L1_EPS / SELU_SCALE)
+            r_l1 = small.tile([P, 4, HALF_HEADS], F32)
+            nc.vector.tensor_reduce(
+                out=r_l1[:].rearrange("p nt h -> p (nt h)"),
+                in_=sums[i][:].rearrange("p (nh o) -> p nh o", o=QUARTER),
+                axis=AXIS.X,
+                op=ALU.add,
+            )
+            nc.vector.tensor_scalar_max(out=r_l1[:], in0=r_l1[:], scalar1=L1_EPS / SELU_SCALE)
             nc.vector.reciprocal(out=r_l1[:], in_=r_l1[:])
-            out_sb = stream.tile([P, 4, 512], F32, tag="stream")
-            for nt in range(4):
-                nc.vector.tensor_tensor(
-                    out=out_sb[:, nt, :].rearrange("p (g e) -> p g e", e=HEAD),
-                    in0=d_ts[i, nt][:].rearrange("p (g e) -> p g e", e=HEAD),
-                    in1=r_l1[:, nt, :].unsqueeze(2).to_broadcast([P, 512 // HEAD, HEAD]),
-                    op=ALU.mult,
-                )
+            r_l1s[i] = r_l1
+
+        def normalise(i, nt):
+            if nt == 0:
+                out_sb = stream.tile([P, 4, 512], F32, tag="stream")
+                outs[i] = out_sb
+            nc.vector.tensor_tensor(
+                out=outs[i][:, nt, :].rearrange("p (h k o) -> p k h o", k=4, o=QUARTER),
+                in0=d_ts[i, nt][:].rearrange("p (k h o) -> p k h o", k=4, o=QUARTER),
+                in1=r_l1s[i][:, nt, :].unsqueeze(1).unsqueeze(3).to_broadcast([P, 4, HALF_HEADS, QUARTER]),
+                op=ALU.mult,
+            )
+
+        def store(i):
+            u, hf = divmod(i, 2)
             first_tile = UNIT * u // P
-            nc.sync.dma_start(out=out_v[:, first_tile : first_tile + 4, 512 * hf : 512 * (hf + 1)], in_=out_sb[:])
+            nc.sync.dma_start(out=out_v[:, first_tile : first_tile + 4, 512 * hf : 512 * (hf + 1)], in_=outs[i][:])
 
         steps = PASSES * ROWS // UNIT
         with tc.manual_schedule():
             linear(0)
-            exponential(0)
+            clamp(0)
             linear(1)
-            exponential(1)
-            combine(0)
-            combine(1)
-            quantise(0)
+            clamp(1)
+            exponential(0)
             linear(2)
+            combine(0)
+            clamp(2)
+            exponential(1)
+            linear(3)
+            quantise(0)
+            combine(1)
+            clamp(3)
             exponential(2)
             quantise(1)
-            linear(3)
-            exponential(3)
+            for k in range(4):
+                product(0, k)
+            branches(0)
             combine(2)
-            for i in range(steps + 2):
-                if i < steps:
-                    for ob4 in range(3):
-                        product(i, ob4)
-                if i + 2 < steps:
-                    quantise(i + 2)
-                if 1 <= i <= steps:
-                    head_selu(i - 1)
-                    magnitudes(i - 1)
-                if i >= 2:
-                    normalise(i - 2)
-                if 1 <= i <= steps:
-                    norms(i - 1)
-                    turn(i - 1)
-                if i < steps:
-                    branches(i, 0)
-                    product(i, 3)
-                    for ob4 in range(1, 4):
-                        branches(i, ob4)
+            exponential(3)
+            linear(4)
+            quantise(2)
+            clamp(4)
+            combine(3)
+            for i in range(steps + 1):
+                now = i < steps
+                before = i >= 1
+                if now:
+                    head_selus(i)
+                if i + 1 < steps:
+                    for k in range(4):
+                        product(i + 1, k)
                 if i + 4 < steps:
-                    linear(i + 4)
                     exponential(i + 4)
+                    combine(i + 4)
+                if i + 5 < steps:
+                    linear(i + 5)
+                if now:
+                    magnitudes(i)
+                if before:
+                    norms(i - 1)
+                    normalise(i - 1, 0)
+                    turn(i - 1, 3)
+                if i + 1 < steps:
+                    branches(i + 1)
+                if before:
+                    for nt in range(1, 4):
+                        normalise(i - 1, nt)
+                    store(i - 1)
+                if now:
+                    turn_magnitudes(i)
+                    for nt in range(3):
+                        turn(i, nt)
+                if i + 5 < steps:
+                    clamp(i + 5)
                 if i + 3 < steps:
-                    combine(i + 3)
+                    quantise(i + 3)

@@ -19,9 +19,9 @@ ROWS = 4096
 HID = 1024
 OUTS = 1024
 HEAD = 32
-QUARTER = HEAD // 4
-HALF_HEADS = 16
-CLAMPED = 2
+BLOCKS = OUTS // P
+HEADS = OUTS // HEAD
+SHARE = P // HEADS
 ROW_TILES = ROWS // P
 WORD_BLOCKS = HID // 2 // P
 PLANES = 2 * WORD_BLOCKS
@@ -31,6 +31,7 @@ LOAD_TILES = 4
 LOAD_COLS = LOAD_TILES * P
 STAT_COLS = 256
 UNIT = 512
+STEP = 256
 
 BN_EPS = 1e-5
 L1_EPS = 1e-12
@@ -53,7 +54,7 @@ def tile_basicemotionpredictions_pa_t_kernel(tc, h2, gamma, beta, Wh, bh, out):
         name="post", bufs=2
     ) as post, tc.tile_pool(name="small", bufs=3) as small, tc.psum_pool(name="psum_mm", bufs=4) as psum_mm, tc.psum_pool(
         name="psum_tr", bufs=3
-    ) as psum_tr, tc.psum_pool(name="psum_abs", bufs=1) as psum_abs:
+    ) as psum_tr, tc.psum_pool(name="psum_sum", bufs=1) as psum_sum:
         warm = keep.tile([P, 1], F32)
         nc.vector.memset(warm[:], 1.0)
         warm_out = keep.tile([P, 1], F32)
@@ -70,26 +71,21 @@ def tile_basicemotionpredictions_pa_t_kernel(tc, h2, gamma, beta, Wh, bh, out):
         beta_sb = keep.tile([P, PASSES, 4], BF16)
         bh_rows = keep.tile([P, P], BF16)
         nc.vector.memset(bh_rows[:], 0.0)
-        bh_v = bh.rearrange("(hf a) g (k o) -> hf k (a g) o", hf=2, k=4)
-        for hf in range(2):
-            nc.scalar.dma_start(
-                out=bh_rows[4 * hf : 4 * (hf + 1), :].rearrange("k (h o) -> k h o", o=QUARTER), in_=bh_v[hf]
-            )
+        nc.scalar.dma_start(
+            out=bh_rows[0:BLOCKS, :].rearrange("k (h o) -> k h o", o=SHARE),
+            in_=bh.rearrange("a g (k o) -> k (a g) o", k=BLOCKS),
+        )
         nc.scalar.dma_start(out=gamma_sb[:], in_=gamma.rearrange("(c q t) -> q c t", c=PASSES, q=P))
         nc.scalar.dma_start(out=beta_sb[:], in_=beta.rearrange("(c q t) -> q c t", c=PASSES, q=P))
 
         bh_f32 = keep.tile([P, P], F32)
         nc.vector.tensor_copy(out=bh_f32[:], in_=bh_rows[:])
-        bh_ps = psum_abs.tile([P, 512], F32, tag="abs")
+        bh_ps = psum_sum.tile([P, 512], F32, tag="sum")
         nc.tensor.transpose(bh_ps[:, 0:P], bh_f32[:], ident[:])
         bias = keep.tile([P, OUTS // P], F32)
         bias_exp = keep.tile([P, OUTS // P], F32)
-        neg_bias = keep.tile([P, OUTS // P], F32)
-        bias_minus = keep.tile([P, OUTS // P], F32)
         nc.vector.tensor_copy(out=bias[:], in_=bh_ps[:, 0 : OUTS // P])
         nc.vector.tensor_scalar_add(out=bias_exp[:], in0=bias[:], scalar1=math.log(SELU_ALPHA))
-        nc.vector.tensor_scalar_mul(out=neg_bias[:], in0=bias[:], scalar1=-1.0)
-        nc.vector.tensor_scalar_add(out=bias_minus[:], in0=bias[:], scalar1=-SELU_ALPHA)
 
         x_t = keep.tile([P, WORD_BLOCKS, ROWS], F32)
         stats = keep.tile([P, WORD_BLOCKS, ROWS // STAT_COLS, 6], F32)
@@ -150,25 +146,27 @@ def tile_basicemotionpredictions_pa_t_kernel(tc, h2, gamma, beta, Wh, bh, out):
             out=b_rel[:], in0=b_neg[:], scalar1=-SELU_SCALE, scalar2=neg_e0[:], op0=ALU.mult, op1=ALU.add
         )
 
-        w_codes = keep.tile([P, 2, PASSES, 512], U32, align_bytes=64)
-        w_scales = keep.tile([P, 2, PASSES, 512], U8, align_bytes=64)
-        for hf in range(2):
+        w_codes = keep.tile([P, PASSES, OUTS], U32, align_bytes=64)
+        w_scales = keep.tile([P, PASSES, OUTS], U8, align_bytes=64)
+        for half in range(2):
             for c in range(PASSES):
-                w_grouped = qin.tile([P, 512, 4], BF16, tag="grouped", align_bytes=64)
+                w_grouped = qin.tile([P, 4, HEADS, SHARE, 4], BF16, tag="grouped", align_bytes=64)
                 for k in range(4):
-                    nc.scalar.copy(
-                        out=w_grouped[:, P * k : P * (k + 1), :].rearrange("q (h o) t -> q h o t", o=QUARTER),
-                        in_=w_raws[hf][:, :, 4 * c : 4 * (c + 1), QUARTER * k : QUARTER * (k + 1)].rearrange(
-                            "q h t o -> q h o t"
-                        ),
-                    )
+                    first = SHARE * (4 * half + k)
+                    for hf in range(2):
+                        nc.scalar.copy(
+                            out=w_grouped[:, k, 16 * hf : 16 * (hf + 1), :, :],
+                            in_=w_raws[hf][:, :, 4 * c : 4 * (c + 1), first : first + SHARE].rearrange(
+                                "q h t o -> q h o t"
+                            ),
+                        )
                 nc.vector.quantize_mx(
-                    out=w_codes[:, hf, c, :].bitcast(FP8X4),
-                    scales=w_scales[:, hf, c, :],
-                    in_=w_grouped[:].rearrange("q o t -> q (o t)"),
+                    out=w_codes[:, c, 512 * half : 512 * (half + 1)].bitcast(FP8X4),
+                    scales=w_scales[:, c, 512 * half : 512 * (half + 1)],
+                    in_=w_grouped[:].rearrange("q k h o t -> q (k h o t)"),
                 )
 
-        e_lins, e_exps, e_groups, e_codes, e_scales = {}, {}, {}, {}, {}
+        e_lins, e_exps, e_planes, e_groups, e_codes, e_scales = {}, {}, {}, {}, {}, {}
 
         def x_plane(p, t):
             u, c = divmod(p, PASSES)
@@ -176,7 +174,7 @@ def tile_basicemotionpredictions_pa_t_kernel(tc, h2, gamma, beta, Wh, bh, out):
             return words.bitcast(BF16).rearrange("q (j e2) -> q j e2", e2=2)[:, :, t % 2]
 
         def linear(p):
-            e_lin = work.tile([P, 4, UNIT], F32)
+            e_lin = work.tile([P, 4, UNIT], F32, bufs=3)
             for t in range(4):
                 plane = 4 * (p % PASSES) + t
                 nc.scalar.activation(
@@ -194,14 +192,17 @@ def tile_basicemotionpredictions_pa_t_kernel(tc, h2, gamma, beta, Wh, bh, out):
             nc.scalar.activation(out=e_exps[p][:], in_=e_exps[p][:], func=ACT.Exp, scale=1.0 / SELU_SCALE, bias=exp_bias[:])
 
         def combine(p):
-            e_group = qin.tile([P, UNIT, 4], BF16, tag="grouped", align_bytes=64)
+            e_plane = work.tile([P, 4, UNIT], BF16)
             nc.vector.scalar_tensor_tensor(
-                out=e_group[:],
-                in0=e_lins[p][:].rearrange("q t j -> q j t"),
-                scalar=neg_e0[:],
-                in1=e_exps[p][:].rearrange("q t j -> q j t"),
-                op0=ALU.max,
-                op1=ALU.add,
+                out=e_plane[:], in0=e_lins[p][:], scalar=neg_e0[:], in1=e_exps[p][:], op0=ALU.max, op1=ALU.add
+            )
+            e_planes[p] = e_plane
+
+        def interleave(p):
+            e_group = qin.tile([P, UNIT, 4], BF16, tag="grouped", align_bytes=64)
+            nc.vector.tensor_copy(
+                out=e_group[:].rearrange("q (r i) t -> q r t i", i=4),
+                in_=e_planes[p][:].rearrange("q t (r i) -> q r t i", i=4),
             )
             e_groups[p] = e_group
 
@@ -217,169 +218,192 @@ def tile_basicemotionpredictions_pa_t_kernel(tc, h2, gamma, beta, Wh, bh, out):
                 in_=e_groups[p][:].rearrange("q j t -> q (j t)"),
             )
 
-        accs, ds, z_rels, d_abss, sums, d_ts, r_l1s, outs = {}, {}, {}, {}, {}, {}, {}, {}
+        accs, z_exps, z_rels, sums, d_ts, r_l1s, outs = {}, {}, {}, {}, {}, {}, {}
 
-        def product(i, k):
-            u, hf = divmod(i, 2)
-            w_cols = slice(P * k, P * (k + 1))
-            acc = psum_mm.tile([P, UNIT], F32)
-            for c in range(PASSES):
-                nc.tensor.matmul_mx(
-                    out=acc[:],
-                    lhsT=w_codes[:, hf, c, w_cols].bitcast(FP8X4),
-                    lhsT_scale=w_scales[:, hf, c, w_cols],
-                    rhs=e_codes[u][:, c, :].bitcast(FP8X4),
-                    rhs_scale=e_scales[u][:, c, :],
-                    start=(c == 0),
-                    stop=(c == PASSES - 1),
+        def product(i, b):
+            u, s = divmod(i, UNIT // STEP)
+            rows = slice(STEP * s, STEP * (s + 1))
+            acc = psum_mm.tile([P, 2, STEP], F32)
+            for k in range(2):
+                w_cols = slice(P * (2 * b + k), P * (2 * b + k + 1))
+                for c in range(PASSES):
+                    nc.tensor.matmul_mx(
+                        out=acc[:, k, :],
+                        lhsT=w_codes[:, c, w_cols].bitcast(FP8X4),
+                        lhsT_scale=w_scales[:, c, w_cols],
+                        rhs=e_codes[u][:, c, rows].bitcast(FP8X4),
+                        rhs_scale=e_scales[u][:, c, rows],
+                        start=(c == 0),
+                        stop=(c == PASSES - 1),
+                    )
+            accs[i, b] = acc
+
+        def branches(i, b):
+            if b == 0:
+                z_exp = post.tile([P, BLOCKS, STEP], F32)
+                z_rel = post.tile([P, BLOCKS, STEP], F32)
+                z_exps[i], z_rels[i] = z_exp, z_rel
+            for k in range(2):
+                ob = 2 * b + k
+                nc.scalar.activation(
+                    out=z_exps[i][:, ob, :], in_=accs[i, b][:, k, :], func=ACT.Exp, bias=bias_exp[:, ob : ob + 1]
                 )
-            accs[i, k] = acc
+                nc.scalar.activation(
+                    out=z_rels[i][:, ob, :], in_=accs[i, b][:, k, :], func=ACT.Relu, bias=bias[:, ob : ob + 1]
+                )
 
-        def branches(i):
-            d = post.tile([P, 4, UNIT], F32)
-            z_rel = post.tile([P, 4 - CLAMPED, UNIT], F32)
-            for k in range(4):
-                ob = 4 * (i % 2) + k
-                nc.scalar.activation(out=d[:, k, :], in_=accs[i, k][:], func=ACT.Exp, bias=bias_exp[:, ob : ob + 1])
-                if k >= CLAMPED:
-                    nc.scalar.activation(
-                        out=z_rel[:, k - CLAMPED, :], in_=accs[i, k][:], func=ACT.Relu, bias=bias[:, ob : ob + 1]
-                    )
-            ds[i], z_rels[i] = d, z_rel
-
-        def head_clamp(i, k):
-            ob = 4 * (i % 2) + k
+        def negative(i, half):
+            part = z_exps[i][:, 4 * half : 4 * (half + 1), :]
             nc.vector.tensor_scalar(
-                out=ds[i][:, k, :], in0=ds[i][:, k, :],
-                scalar1=SELU_ALPHA, scalar2=bias_minus[:, ob : ob + 1], op0=ALU.min, op1=ALU.add,
+                out=part, in0=part, scalar1=SELU_ALPHA, scalar2=-SELU_ALPHA, op0=ALU.min, op1=ALU.add
             )
 
-        def head_selu(i, k):
-            ob = 4 * (i % 2) + k
-            nc.vector.scalar_tensor_tensor(
-                out=ds[i][:, k, :], in0=accs[i, k][:], scalar=neg_bias[:, ob : ob + 1], in1=ds[i][:, k, :],
-                op0=ALU.max, op1=ALU.add,
-            )
+        def turn_add(out, sources):
+            for n, source in enumerate(sources):
+                nc.tensor.matmul(
+                    out, lhsT=source, rhs=ident[:], start=(n == 0), stop=(n == len(sources) - 1), is_transpose=True
+                )
 
-        def head_selus(i):
-            for k in range(CLAMPED):
-                head_clamp(i, k)
-            for k in range(CLAMPED):
-                head_selu(i, k)
-            nc.vector.scalar_tensor_tensor(
-                out=ds[i][:, CLAMPED:, :], in0=ds[i][:, CLAMPED:, :], scalar=-SELU_ALPHA, in1=z_rels[i][:],
-                op0=ALU.add, op1=ALU.min,
-            )
+        def branch_sums(i, branch):
+            if branch == 0:
+                total = psum_sum.tile([P, 2, STEP // P, P], F32, tag="sum")
+                sums[i] = total
+            z = (z_rels if branch == 0 else z_exps)[i]
+            for nt in range(STEP // P):
+                turn_add(sums[i][:, branch, nt, :], [z[:, k, P * nt : P * (nt + 1)] for k in range(BLOCKS)])
 
-        def magnitudes(i):
-            d_abs = post.tile([P, 4, UNIT], F32)
-            nc.scalar.activation(out=d_abs[:], in_=ds[i][:], func=ACT.Abs)
-            d_abss[i] = d_abs
-
-        def turn(i, nt):
-            d_t = psum_tr.tile([P, 512], F32, tag="tr")
+        def turn(i, nt, half):
+            d_t = psum_tr.tile([P, 4, P], F32, tag="tr")
             for k in range(4):
-                nc.tensor.transpose(d_t[:, P * k : P * (k + 1)], ds[i][:, k, P * nt : P * (nt + 1)], ident[:])
-            d_ts[i, nt] = d_t
+                ob = 4 * half + k
+                turn_add(d_t[:, k, :], [z[i][:, ob, P * nt : P * (nt + 1)] for z in (z_rels, z_exps)])
+            d_ts[i, nt, half] = d_t
 
-        def turn_magnitudes(i):
-            total = psum_abs.tile([P, 512], F32, tag="abs")
-            for nt in range(4):
-                for k in range(4):
-                    nc.tensor.matmul(
-                        total[:, P * nt : P * (nt + 1)],
-                        lhsT=d_abss[i][:, k, P * nt : P * (nt + 1)],
-                        rhs=ident[:],
-                        start=(k == 0),
-                        stop=(k == 3),
-                        is_transpose=True,
-                    )
-            sums[i] = total
+        parts, l1s = {}, {}
 
-        def norms(i):
-            r_l1 = small.tile([P, 4, HALF_HEADS], F32)
+        def head_sums(i):
+            part = small.tile([P, 2, STEP // P, HEADS], F32)
             nc.vector.tensor_reduce(
-                out=r_l1[:].rearrange("p nt h -> p (nt h)"),
-                in_=sums[i][:].rearrange("p (nh o) -> p nh o", o=QUARTER),
+                out=part[:].rearrange("p b nt h -> p (b nt h)"),
+                in_=sums[i][:].rearrange("p b nt (h o) -> p (b nt h) o", o=SHARE),
                 axis=AXIS.X,
                 op=ALU.add,
             )
-            nc.vector.tensor_scalar_max(out=r_l1[:], in0=r_l1[:], scalar1=L1_EPS / SELU_SCALE)
-            nc.vector.reciprocal(out=r_l1[:], in_=r_l1[:])
+            parts[i] = part
+
+        def norms(i):
+            l1 = small.tile([P, STEP // P, HEADS], F32)
+            nc.vector.scalar_tensor_tensor(
+                out=l1[:], in0=parts[i][:, 0], scalar=L1_EPS / SELU_SCALE, in1=parts[i][:, 1],
+                op0=ALU.max, op1=ALU.subtract,
+            )
+            l1s[i] = l1
+
+        def inverses(i):
+            r_l1 = small.tile([P, STEP // P, HEADS], F32)
+            nc.vector.reciprocal(out=r_l1[:], in_=l1s[i][:])
             r_l1s[i] = r_l1
 
-        def normalise(i, nt):
-            if nt == 0:
-                out_sb = stream.tile([P, 4, 512], F32, tag="stream")
+        def normalise(i, nt, half):
+            if nt == 0 and half == 0:
+                out_sb = stream.tile([P, STEP // P, HEADS, BLOCKS, SHARE], F32, tag="stream")
                 outs[i] = out_sb
             nc.vector.tensor_tensor(
-                out=outs[i][:, nt, :].rearrange("p (h k o) -> p k h o", k=4, o=QUARTER),
-                in0=d_ts[i, nt][:].rearrange("p (k h o) -> p k h o", k=4, o=QUARTER),
-                in1=r_l1s[i][:, nt, :].unsqueeze(1).unsqueeze(3).to_broadcast([P, 4, HALF_HEADS, QUARTER]),
+                out=outs[i][:, nt, :, 4 * half : 4 * (half + 1), :].rearrange("p h k o -> p k h o"),
+                in0=d_ts[i, nt, half][:].rearrange("p k (h o) -> p k h o", o=SHARE),
+                in1=r_l1s[i][:, nt, :].unsqueeze(1).unsqueeze(3).to_broadcast([P, 4, HEADS, SHARE]),
                 op=ALU.mult,
             )
 
         def store(i):
-            u, hf = divmod(i, 2)
-            first_tile = UNIT * u // P
-            nc.sync.dma_start(out=out_v[:, first_tile : first_tile + 4, 512 * hf : 512 * (hf + 1)], in_=outs[i][:])
+            tiles = slice(i * STEP // P, (i + 1) * STEP // P)
+            nc.sync.dma_start(out=out_v[:, tiles, :], in_=outs[i][:].rearrange("p nt h k o -> p nt (h k o)"))
 
-        steps = PASSES * ROWS // UNIT
+        passes = PASSES * ROWS // UNIT
+        steps = ROWS // STEP
         with tc.manual_schedule():
             linear(0)
-            clamp(0)
             linear(1)
-            clamp(1)
-            exponential(0)
+            clamp(0)
             linear(2)
+            exponential(0)
+            clamp(1)
             combine(0)
-            clamp(2)
             exponential(1)
             linear(3)
-            quantise(0)
+            interleave(0)
+            clamp(2)
             combine(1)
-            clamp(3)
+            quantise(0)
             exponential(2)
-            quantise(1)
-            for k in range(4):
-                product(0, k)
-            branches(0)
-            combine(2)
-            exponential(3)
+            interleave(1)
             linear(4)
-            quantise(2)
-            clamp(4)
-            combine(3)
+            clamp(3)
+            combine(2)
+            quantise(1)
+            product(0, 0)
+            product(0, 1)
+            product(0, 2)
+            product(0, 3)
+            interleave(2)
             for i in range(steps + 1):
-                now = i < steps
-                before = i >= 1
-                if now:
-                    head_selus(i)
-                if i + 1 < steps:
-                    for k in range(4):
-                        product(i + 1, k)
-                if i + 4 < steps:
-                    exponential(i + 4)
-                    combine(i + 4)
-                if i + 5 < steps:
-                    linear(i + 5)
-                if now:
-                    magnitudes(i)
-                if before:
+                if 0 <= i + 2 < passes:
+                    quantise(i + 2)
+                if 0 <= i + 4 < passes:
+                    clamp(i + 4)
+                if 0 <= i + 3 < passes:
+                    exponential(i + 3)
+                if 0 <= i < steps:
+                    branches(i, 0)
+                if 0 <= i + 1 < steps:
+                    product(i + 1, 0)
+                if 0 <= i < steps:
+                    branches(i, 1)
+                if 0 <= i + 1 < steps:
+                    product(i + 1, 1)
+                if 0 <= i + 3 < passes:
+                    combine(i + 3)
+                if 0 <= i - 1 < steps:
+                    head_sums(i - 1)
+                if 0 <= i - 1 < steps:
                     norms(i - 1)
-                    normalise(i - 1, 0)
-                    turn(i - 1, 3)
-                if i + 1 < steps:
-                    branches(i + 1)
-                if before:
-                    for nt in range(1, 4):
-                        normalise(i - 1, nt)
+                if 0 <= i + 3 < passes:
+                    interleave(i + 3)
+                if 0 <= i - 1 < steps:
+                    inverses(i - 1)
+                if 0 <= i < steps:
+                    branches(i, 2)
+                if 0 <= i + 1 < steps:
+                    product(i + 1, 2)
+                if 0 <= i < steps:
+                    branches(i, 3)
+                if 0 <= i + 1 < steps:
+                    product(i + 1, 3)
+                if 0 <= i + 5 < passes:
+                    linear(i + 5)
+                if 0 <= i - 1 < steps:
+                    normalise(i - 1, 0, 0)
+                if 0 <= i - 1 < steps:
+                    turn(i - 1, 1, 1)
+                if 0 <= i < steps:
+                    branch_sums(i, 0)
+                if 0 <= i < steps:
+                    negative(i, 0)
+                if 0 <= i - 1 < steps:
+                    normalise(i - 1, 0, 1)
+                if 0 <= i < steps:
+                    negative(i, 1)
+                if 0 <= i < steps:
+                    branch_sums(i, 1)
+                if 0 <= i < steps:
+                    turn(i, 0, 0)
+                if 0 <= i - 1 < steps:
+                    normalise(i - 1, 1, 0)
+                if 0 <= i < steps:
+                    turn(i, 0, 1)
+                if 0 <= i - 1 < steps:
+                    normalise(i - 1, 1, 1)
+                if 0 <= i < steps:
+                    turn(i, 1, 0)
+                if 0 <= i - 1 < steps:
                     store(i - 1)
-                if now:
-                    turn_magnitudes(i)
-                    for nt in range(3):
-                        turn(i, nt)
-                if i + 5 < steps:
-                    clamp(i + 5)
-                if i + 3 < steps:
-                    quantise(i + 3)

@@ -1,4 +1,5 @@
 import math
+from contextlib import ExitStack
 
 import concourse.bass as bass
 import concourse.mybir as mybir
@@ -23,13 +24,15 @@ BLOCKS = OUTS // P
 HEADS = OUTS // HEAD
 SHARE = P // HEADS
 ROW_TILES = ROWS // P
-WORD_BLOCKS = HID // 2 // P
-PLANES = 2 * WORD_BLOCKS
-PASSES = HID // 512
+K_PASS = 512
+PASSES = HID // K_PASS
+PLANES = 4 * PASSES
 
 LOAD_TILES = 4
 LOAD_COLS = LOAD_TILES * P
+ROW_COLS = HID + 16
 STAT_COLS = 256
+ON_VECTOR = 1
 UNIT = 512
 STEP = 256
 
@@ -48,22 +51,32 @@ def tile_basicemotionpredictions_pa_t_kernel(tc, h2, gamma, beta, Wh, bh, out):
     out_v = out.rearrange("(p n) h g e -> p n (h g e)", n=ROW_TILES)
     wh_v = Wh.rearrange("h g (c q t) e -> q (h g c) (t e)", c=PASSES, q=P, t=4)
 
-    with tc.tile_pool(name="keep", bufs=1) as keep, tc.tile_pool(name="stream", bufs=3) as stream, tc.tile_pool(
-        name="qin", bufs=2
-    ) as qin, tc.tile_pool(name="work", bufs=2) as work, tc.tile_pool(name="codes", bufs=3) as codes, tc.tile_pool(
-        name="post", bufs=2
-    ) as post, tc.tile_pool(name="small", bufs=3) as small, tc.psum_pool(name="psum_mm", bufs=4) as psum_mm, tc.psum_pool(
-        name="psum_tr", bufs=3
-    ) as psum_tr, tc.psum_pool(name="psum_sum", bufs=1) as psum_sum:
-        warm = keep.tile([P, 1], F32)
-        nc.vector.memset(warm[:], 1.0)
-        warm_out = keep.tile([P, 1], F32)
-        nc.scalar.activation(out=warm_out[:], in_=warm[:], func=ACT.Sqrt)
+    with ExitStack() as ctx:
+        keep = ctx.enter_context(tc.tile_pool(name="keep", bufs=1))
+        big = ctx.enter_context(tc.tile_pool(name="big", bufs=8))
+        qin = ctx.enter_context(tc.tile_pool(name="qin", bufs=3))
+        wraw = ctx.enter_context(tc.tile_pool(name="wraw", bufs=2))
+        work = ctx.enter_context(tc.tile_pool(name="work", bufs=2))
+        codes = ctx.enter_context(tc.tile_pool(name="codes", bufs=3))
+        small = ctx.enter_context(tc.tile_pool(name="small", bufs=3))
+        psum_mm = ctx.enter_context(tc.psum_pool(name="psum_mm", bufs=4))
+        psum_tr = ctx.enter_context(tc.psum_pool(name="psum_tr", bufs=3))
+        psum_sum = ctx.enter_context(tc.psum_pool(name="psum_sum", bufs=1))
+        ctx.enter_context(tc.manual_schedule())
+
         zero = keep.tile([P, 1], F32)
         nc.vector.memset(zero[:], 0.0)
+        minus_half = keep.tile([P, PASSES, 4], F32)
+        nc.vector.memset(minus_half[:], -0.5)
         ln_sa = keep.tile([P, 1], F32)
         nc.vector.tensor_scalar_add(out=ln_sa[:], in0=zero[:], scalar1=math.log(SA))
-
+        neg_e0 = keep.tile([P, 1], F32)
+        nc.scalar.activation(out=neg_e0[:], in_=zero[:], func=ACT.Exp, bias=ln_sa[:])
+        nc.vector.tensor_scalar_mul(out=neg_e0[:], in0=neg_e0[:], scalar1=-1.0)
+        exp_bias = keep.tile([P, 1], F32)
+        nc.vector.tensor_scalar(
+            out=exp_bias[:], in0=neg_e0[:], scalar1=-1.0 / SELU_SCALE, scalar2=math.log(SA), op0=ALU.mult, op1=ALU.add
+        )
         ident = keep.tile([P, P], F32)
         make_identity(nc, ident[:])
 
@@ -78,6 +91,53 @@ def tile_basicemotionpredictions_pa_t_kernel(tc, h2, gamma, beta, Wh, bh, out):
         nc.scalar.dma_start(out=gamma_sb[:], in_=gamma.rearrange("(c q t) -> q c t", c=PASSES, q=P))
         nc.scalar.dma_start(out=beta_sb[:], in_=beta.rearrange("(c q t) -> q c t", c=PASSES, q=P))
 
+        x_t = keep.tile([P, PASSES, 2, ROWS], F32)
+        stats = keep.tile([P, 2, ROWS // STAT_COLS, 6], F32)
+
+        def turn_load(c, ld):
+            for w in range(2):
+                xt_ps = psum_tr.tile([P, LOAD_COLS], F32, tag="tr")
+                for i in range(LOAD_TILES):
+                    words = loads[ld][:, i, K_PASS * c : K_PASS * (c + 1)].bitcast(F32)
+                    nc.tensor.transpose(xt_ps[:, P * i : P * (i + 1)], words[:, w::2], ident[:])
+                nc.scalar.copy(out=x_t[:, c, w, LOAD_COLS * ld : LOAD_COLS * (ld + 1)], in_=xt_ps[:])
+
+        def statistics(ld):
+            for w in range(2):
+                for s in range(LOAD_COLS // STAT_COLS):
+                    first = LOAD_COLS * ld + STAT_COLS * s
+                    nc.vector.bn_stats(
+                        out=stats[:, w, first // STAT_COLS, :],
+                        in_=x_t[:, 0, w, first : first + STAT_COLS].bitcast(BF16),
+                    )
+
+        def gram(ld):
+            for i in range(LOAD_TILES):
+                for t in range(4):
+                    if ld == 0 and i == 0:
+                        bank = psum_mm.tile([P, LOAD_COLS], F32, tag="mm")
+                        grams.append(bank)
+                    row = loads[ld][:, i, :]
+                    nc.tensor.matmul(
+                        grams[t][:, 0 : P + 1],
+                        lhsT=row[:, K_PASS + t : HID : 4],
+                        rhs=row[:, K_PASS + t : HID + 4 : 4],
+                        start=(ld == 0 and i == 0),
+                        stop=(ld == n_loads - 1 and i == LOAD_TILES - 1),
+                    )
+
+        loads, grams = [], []
+        n_loads = ROW_TILES // LOAD_TILES
+        for ld in range(n_loads):
+            x_sb = big.tile([P, LOAD_TILES, ROW_COLS], BF16, tag="big")
+            nc.vector.memset(x_sb[:, :, HID:], 1.0)
+            nc.sync.dma_start(out=x_sb[:, :, 0:HID], in_=h2_v[:, LOAD_TILES * ld : LOAD_TILES * (ld + 1), :])
+            loads.append(x_sb)
+        turn_load(0, 0)
+        statistics(0)
+        gram(0)
+        turn_load(0, 1)
+        statistics(1)
         bh_f32 = keep.tile([P, P], F32)
         nc.vector.tensor_copy(out=bh_f32[:], in_=bh_rows[:])
         bh_ps = psum_sum.tile([P, 512], F32, tag="sum")
@@ -87,127 +147,118 @@ def tile_basicemotionpredictions_pa_t_kernel(tc, h2, gamma, beta, Wh, bh, out):
         nc.vector.tensor_copy(out=bias[:], in_=bh_ps[:, 0 : OUTS // P])
         nc.vector.tensor_scalar_add(out=bias_exp[:], in0=bias[:], scalar1=math.log(SELU_ALPHA))
 
-        x_t = keep.tile([P, WORD_BLOCKS, ROWS], F32)
-        stats = keep.tile([P, WORD_BLOCKS, ROWS // STAT_COLS, 6], F32)
-        for ld in range(ROW_TILES // LOAD_TILES):
-            x_sb = stream.tile([P, LOAD_TILES, HID], BF16, tag="stream")
-            nc.sync.dma_start(out=x_sb[:], in_=h2_v[:, LOAD_TILES * ld : LOAD_TILES * (ld + 1), :])
-            for wb in range(WORD_BLOCKS):
-                xt_ps = psum_tr.tile([P, LOAD_COLS], F32, tag="tr")
-                for i in range(LOAD_TILES):
-                    nc.tensor.transpose(
-                        xt_ps[:, P * i : P * (i + 1)],
-                        x_sb[:, i, :].bitcast(F32)[:, 256 * (wb // 2) + wb % 2 : 256 * (wb // 2 + 1) : 2],
-                        ident[:],
-                    )
-                nc.scalar.copy(out=x_t[:, wb, LOAD_COLS * ld : LOAD_COLS * (ld + 1)], in_=xt_ps[:])
-                for s in range(LOAD_COLS // STAT_COLS):
-                    first = LOAD_COLS * ld + STAT_COLS * s
-                    nc.vector.bn_stats(
-                        out=stats[:, wb, first // STAT_COLS, :],
-                        in_=x_t[:, wb, first : first + STAT_COLS].bitcast(BF16),
-                    )
+        gram(1)
+        for ld in range(2, n_loads):
+            turn_load(0, ld)
+            statistics(ld)
+            gram(ld)
 
         w_raws = []
         for hf in range(2):
-            w_raw = stream.tile([P, 16, PLANES, HEAD], BF16, tag="stream")
+            w_raw = wraw.tile([P, 16, PLANES, HEAD], BF16)
             nc.sync.dma_start(
                 out=w_raw[:].rearrange("q hg (c t) e -> q (hg c) (t e)", t=4),
                 in_=wh_v[:, 32 * hf : 32 * (hf + 1), :],
             )
             w_raws.append(w_raw)
 
-        mv = keep.tile([P, PLANES, 2], F32)
-        for wb in range(WORD_BLOCKS):
-            for e2 in range(2):
-                nc.vector.bn_aggr(out=mv[:, 2 * wb + e2, :], in_=stats[:, wb, :, 3 * e2 : 3 * e2 + 3])
-        var_eps = keep.tile([P, PLANES], F32)
-        std = keep.tile([P, PLANES], F32)
-        rstd = keep.tile([P, PLANES], F32)
-        a_lin = keep.tile([P, PLANES], F32)
-        b_neg = keep.tile([P, PLANES], F32)
-        a_rel = keep.tile([P, PLANES], F32)
-        b_rel = keep.tile([P, PLANES], F32)
-        nc.vector.tensor_scalar_add(out=var_eps[:], in0=mv[:, :, 1], scalar1=BN_EPS)
-        nc.scalar.activation(out=std[:], in_=var_eps[:], func=ACT.Sqrt)
-        nc.vector.reciprocal(out=rstd[:], in_=std[:])
-        nc.vector.tensor_tensor(out=a_lin[:], in0=gamma_sb[:].rearrange("q c t -> q (c t)"), in1=rstd[:], op=ALU.mult)
-        nc.vector.tensor_tensor(out=b_neg[:], in0=mv[:, :, 0], in1=a_lin[:], op=ALU.mult)
-        nc.vector.tensor_tensor(out=b_neg[:], in0=b_neg[:], in1=beta_sb[:].rearrange("q c t -> q (c t)"), op=ALU.subtract)
-        nc.vector.tensor_scalar_mul(out=a_rel[:], in0=a_lin[:], scalar1=SELU_SCALE)
-        neg_e0 = keep.tile([P, 1], F32)
-        nc.scalar.activation(out=neg_e0[:], in_=zero[:], func=ACT.Exp, bias=ln_sa[:])
-        nc.vector.tensor_scalar_mul(out=neg_e0[:], in0=neg_e0[:], scalar1=-1.0)
-        exp_bias = keep.tile([P, 1], F32)
+        gamma_s = keep.tile([P, PASSES, 4], F32)
+        beta_s = keep.tile([P, PASSES, 4], F32)
+        nc.vector.tensor_scalar_mul(out=gamma_s[:], in0=gamma_sb[:], scalar1=SELU_SCALE)
         nc.vector.tensor_scalar(
-            out=exp_bias[:], in0=neg_e0[:], scalar1=-1.0 / SELU_SCALE, scalar2=math.log(SA), op0=ALU.mult, op1=ALU.add
+            out=beta_s[:], in0=beta_sb[:], scalar1=SELU_SCALE, scalar2=neg_e0[:], op0=ALU.mult, op1=ALU.add
         )
-        nc.vector.tensor_scalar(
-            out=b_rel[:], in0=b_neg[:], scalar1=-SELU_SCALE, scalar2=neg_e0[:], op0=ALU.mult, op1=ALU.add
-        )
+        a_rel = keep.tile([P, PASSES, 4], F32)
+        b_rel = keep.tile([P, PASSES, 4], F32)
+
+        def scale_and_bias():
+            mean = keep.tile([P, PASSES, 4], F32)
+            var = keep.tile([P, PASSES, 4], F32)
+            mv = small.tile([P, 4, 2], F32)
+            for t in range(4):
+                nc.vector.bn_aggr(out=mv[:, t, :], in_=stats[:, t // 2, :, 3 * (t % 2) : 3 * (t % 2) + 3])
+            nc.vector.tensor_copy(out=mean[:, 0, :], in_=mv[:, :, 0])
+            nc.vector.tensor_copy(out=var[:, 0, :], in_=mv[:, :, 1])
+            square = small.tile([P, 4], F32)
+            for t in range(4):
+                junk = small.tile([P, P], F32)
+                nc.vector.tensor_scalar_mul(out=mean[:, 1, t : t + 1], in0=grams[t][:, P : P + 1], scalar1=1.0 / ROWS)
+                nc.vector.scalar_tensor_tensor(
+                    out=junk[:], in0=grams[t][:, 0:P], scalar=1.0 / ROWS, in1=ident[:],
+                    op0=ALU.mult, op1=ALU.mult, accum_out=square[:, t : t + 1],
+                )
+            square_of_mean = small.tile([P, 4], F32)
+            nc.vector.tensor_tensor(out=square_of_mean[:], in0=mean[:, 1, :], in1=mean[:, 1, :], op=ALU.mult)
+            nc.vector.tensor_tensor(out=var[:, 1, :], in0=square[:], in1=square_of_mean[:], op=ALU.subtract)
+            nc.vector.tensor_scalar(out=var[:], in0=var[:], scalar1=0.0, scalar2=BN_EPS, op0=ALU.max, op1=ALU.add)
+            rstd = keep.tile([P, PASSES, 4], F32)
+            nc.gpsimd.tensor_tensor(out=rstd[:], in0=var[:], in1=minus_half[:], op=ALU.pow)
+            nc.vector.tensor_tensor(out=a_rel[:], in0=gamma_s[:], in1=rstd[:], op=ALU.mult)
+            nc.vector.tensor_tensor(out=mean[:], in0=mean[:], in1=a_rel[:], op=ALU.mult)
+            nc.vector.tensor_tensor(out=b_rel[:], in0=beta_s[:], in1=mean[:], op=ALU.subtract)
 
         w_codes = keep.tile([P, PASSES, OUTS], U32, align_bytes=64)
         w_scales = keep.tile([P, PASSES, OUTS], U8, align_bytes=64)
-        for half in range(2):
-            for c in range(PASSES):
-                w_grouped = qin.tile([P, 4, HEADS, SHARE, 4], BF16, tag="grouped", align_bytes=64)
-                for k in range(4):
-                    first = SHARE * (4 * half + k)
-                    for hf in range(2):
-                        nc.scalar.copy(
-                            out=w_grouped[:, k, 16 * hf : 16 * (hf + 1), :, :],
-                            in_=w_raws[hf][:, :, 4 * c : 4 * (c + 1), first : first + SHARE].rearrange(
-                                "q h t o -> q h o t"
-                            ),
-                        )
-                nc.vector.quantize_mx(
-                    out=w_codes[:, c, 512 * half : 512 * (half + 1)].bitcast(FP8X4),
-                    scales=w_scales[:, c, 512 * half : 512 * (half + 1)],
-                    in_=w_grouped[:].rearrange("q k h o t -> q (k h o t)"),
-                )
+        w_groups = {}
 
-        e_lins, e_exps, e_planes, e_groups, e_codes, e_scales = {}, {}, {}, {}, {}, {}
+        def regroup_weights(half, c):
+            w_grouped = qin.tile([P, 4, HEADS, SHARE, 4], BF16, tag="grouped", align_bytes=64)
+            for k in range(4):
+                first = SHARE * (4 * half + k)
+                for hf in range(2):
+                    nc.vector.tensor_copy(
+                        out=w_grouped[:, k, 16 * hf : 16 * (hf + 1), :, :],
+                        in_=w_raws[hf][:, :, 4 * c : 4 * (c + 1), first : first + SHARE].rearrange("q h t o -> q h o t"),
+                    )
+            w_groups[half, c] = w_grouped
 
-        def x_plane(p, t):
-            u, c = divmod(p, PASSES)
-            words = x_t[:, 2 * c + t // 2, UNIT * u : UNIT * (u + 1)]
-            return words.bitcast(BF16).rearrange("q (j e2) -> q j e2", e2=2)[:, :, t % 2]
+        def quantise_weights(half, c):
+            nc.vector.quantize_mx(
+                out=w_codes[:, c, 512 * half : 512 * (half + 1)].bitcast(FP8X4),
+                scales=w_scales[:, c, 512 * half : 512 * (half + 1)],
+                in_=w_groups[half, c][:].rearrange("q k h o t -> q (k h o t)"),
+            )
 
-        def linear(p):
+        tiles = [(u, c) for u in range(ROWS // UNIT) for c in range(PASSES)]
+        e_lins, e_exps, e_groups, e_codes, e_scales = {}, {}, {}, {}, {}
+
+        def linear(n):
+            u, c = tiles[n]
             e_lin = work.tile([P, 4, UNIT], F32, bufs=3)
             for t in range(4):
-                plane = 4 * (p % PASSES) + t
-                nc.scalar.activation(
-                    out=e_lin[:, t, :], in_=x_plane(p, t), func=ACT.Identity,
-                    scale=a_rel[:, plane : plane + 1], bias=b_rel[:, plane : plane + 1],
-                )
-            e_lins[p] = e_lin
+                words = x_t[:, c, t // 2, UNIT * u : UNIT * (u + 1)]
+                x_plane = words.bitcast(BF16).rearrange("q (j e2) -> q j e2", e2=2)[:, :, t % 2]
+                scale, shift = a_rel[:, c, t : t + 1], b_rel[:, c, t : t + 1]
+                if t < 4 - ON_VECTOR:
+                    nc.scalar.activation(out=e_lin[:, t, :], in_=x_plane, func=ACT.Identity, scale=scale, bias=shift)
+                else:
+                    nc.vector.tensor_scalar(
+                        out=e_lin[:, t, :], in0=x_plane, scalar1=scale, scalar2=shift, op0=ALU.mult, op1=ALU.add
+                    )
+            e_lins[n] = e_lin
 
-        def clamp(p):
+        def clamp(n):
             e_exp = work.tile([P, 4, UNIT], F32)
-            nc.vector.tensor_scalar(out=e_exp[:], in0=e_lins[p][:], scalar1=neg_e0[:], scalar2=None, op0=ALU.min)
-            e_exps[p] = e_exp
+            nc.vector.tensor_scalar(out=e_exp[:], in0=e_lins[n][:], scalar1=neg_e0[:], scalar2=None, op0=ALU.min)
+            e_exps[n] = e_exp
 
-        def exponential(p):
-            nc.scalar.activation(out=e_exps[p][:], in_=e_exps[p][:], func=ACT.Exp, scale=1.0 / SELU_SCALE, bias=exp_bias[:])
+        def exponential(n):
+            nc.scalar.activation(out=e_exps[n][:], in_=e_exps[n][:], func=ACT.Exp, scale=1.0 / SELU_SCALE, bias=exp_bias[:])
 
-        def combine(p):
-            e_plane = work.tile([P, 4, UNIT], BF16)
-            nc.vector.scalar_tensor_tensor(
-                out=e_plane[:], in0=e_lins[p][:], scalar=neg_e0[:], in1=e_exps[p][:], op0=ALU.max, op1=ALU.add
-            )
-            e_planes[p] = e_plane
-
-        def interleave(p):
+        def combine(n):
             e_group = qin.tile([P, UNIT, 4], BF16, tag="grouped", align_bytes=64)
-            nc.vector.tensor_copy(
-                out=e_group[:].rearrange("q (r i) t -> q r t i", i=4),
-                in_=e_planes[p][:].rearrange("q t (r i) -> q r t i", i=4),
+            nc.vector.scalar_tensor_tensor(
+                out=e_group[:],
+                in0=e_lins[n][:].rearrange("q t j -> q j t"),
+                scalar=neg_e0[:],
+                in1=e_exps[n][:].rearrange("q t j -> q j t"),
+                op0=ALU.max,
+                op1=ALU.add,
             )
-            e_groups[p] = e_group
+            e_groups[n] = e_group
 
-        def quantise(p):
-            u, c = divmod(p, PASSES)
+        def quantise(n):
+            u, c = tiles[n]
             if c == 0:
                 codes_u = codes.tile([P, PASSES, UNIT], U32, align_bytes=64)
                 scales_u = codes.tile([P, PASSES, UNIT], U8, align_bytes=64)
@@ -215,7 +266,7 @@ def tile_basicemotionpredictions_pa_t_kernel(tc, h2, gamma, beta, Wh, bh, out):
             nc.vector.quantize_mx(
                 out=e_codes[u][:, c, :].bitcast(FP8X4),
                 scales=e_scales[u][:, c, :],
-                in_=e_groups[p][:].rearrange("q j t -> q (j t)"),
+                in_=e_groups[n][:].rearrange("q j t -> q (j t)"),
             )
 
         accs, z_exps, z_rels, sums, d_ts, r_l1s, outs = {}, {}, {}, {}, {}, {}, {}
@@ -223,7 +274,7 @@ def tile_basicemotionpredictions_pa_t_kernel(tc, h2, gamma, beta, Wh, bh, out):
         def product(i, b):
             u, s = divmod(i, UNIT // STEP)
             rows = slice(STEP * s, STEP * (s + 1))
-            acc = psum_mm.tile([P, 2, STEP], F32)
+            acc = psum_mm.tile([P, 2, STEP], F32, tag="mm")
             for k in range(2):
                 w_cols = slice(P * (2 * b + k), P * (2 * b + k + 1))
                 for c in range(PASSES):
@@ -240,8 +291,8 @@ def tile_basicemotionpredictions_pa_t_kernel(tc, h2, gamma, beta, Wh, bh, out):
 
         def branches(i, b):
             if b == 0:
-                z_exp = post.tile([P, BLOCKS, STEP], F32)
-                z_rel = post.tile([P, BLOCKS, STEP], F32)
+                z_exp = big.tile([P, BLOCKS, STEP], F32, tag="big")
+                z_rel = big.tile([P, BLOCKS, STEP], F32, tag="big")
                 z_exps[i], z_rels[i] = z_exp, z_rel
             for k in range(2):
                 ob = 2 * b + k
@@ -306,7 +357,7 @@ def tile_basicemotionpredictions_pa_t_kernel(tc, h2, gamma, beta, Wh, bh, out):
 
         def normalise(i, nt, half):
             if nt == 0 and half == 0:
-                out_sb = stream.tile([P, STEP // P, HEADS, BLOCKS, SHARE], F32, tag="stream")
+                out_sb = big.tile([P, STEP // P, HEADS, BLOCKS, SHARE], F32, tag="big")
                 outs[i] = out_sb
             nc.vector.tensor_tensor(
                 out=outs[i][:, nt, :, 4 * half : 4 * (half + 1), :].rearrange("p h k o -> p k h o"),
@@ -319,91 +370,84 @@ def tile_basicemotionpredictions_pa_t_kernel(tc, h2, gamma, beta, Wh, bh, out):
             tiles = slice(i * STEP // P, (i + 1) * STEP // P)
             nc.sync.dma_start(out=out_v[:, tiles, :], in_=outs[i][:].rearrange("p nt h k o -> p nt (h k o)"))
 
-        passes = PASSES * ROWS // UNIT
+        passes = len(tiles)
         steps = ROWS // STEP
-        with tc.manual_schedule():
-            linear(0)
-            linear(1)
-            clamp(0)
-            linear(2)
-            exponential(0)
-            clamp(1)
-            combine(0)
-            exponential(1)
-            linear(3)
-            interleave(0)
-            clamp(2)
-            combine(1)
-            quantise(0)
-            exponential(2)
-            interleave(1)
-            linear(4)
-            clamp(3)
-            combine(2)
-            quantise(1)
-            product(0, 0)
-            product(0, 1)
-            product(0, 2)
-            product(0, 3)
-            interleave(2)
-            for i in range(steps + 1):
-                if 0 <= i + 2 < passes:
-                    quantise(i + 2)
-                if 0 <= i + 4 < passes:
-                    clamp(i + 4)
-                if 0 <= i + 3 < passes:
-                    exponential(i + 3)
-                if 0 <= i < steps:
-                    branches(i, 0)
-                if 0 <= i + 1 < steps:
-                    product(i + 1, 0)
-                if 0 <= i < steps:
-                    branches(i, 1)
-                if 0 <= i + 1 < steps:
-                    product(i + 1, 1)
-                if 0 <= i + 3 < passes:
-                    combine(i + 3)
-                if 0 <= i - 1 < steps:
-                    head_sums(i - 1)
-                if 0 <= i - 1 < steps:
-                    norms(i - 1)
-                if 0 <= i + 3 < passes:
-                    interleave(i + 3)
-                if 0 <= i - 1 < steps:
-                    inverses(i - 1)
-                if 0 <= i < steps:
-                    branches(i, 2)
-                if 0 <= i + 1 < steps:
-                    product(i + 1, 2)
-                if 0 <= i < steps:
-                    branches(i, 3)
-                if 0 <= i + 1 < steps:
-                    product(i + 1, 3)
-                if 0 <= i + 5 < passes:
-                    linear(i + 5)
-                if 0 <= i - 1 < steps:
-                    normalise(i - 1, 0, 0)
-                if 0 <= i - 1 < steps:
-                    turn(i - 1, 1, 1)
-                if 0 <= i < steps:
-                    branch_sums(i, 0)
-                if 0 <= i < steps:
-                    negative(i, 0)
-                if 0 <= i - 1 < steps:
-                    normalise(i - 1, 0, 1)
-                if 0 <= i < steps:
-                    negative(i, 1)
-                if 0 <= i < steps:
-                    branch_sums(i, 1)
-                if 0 <= i < steps:
-                    turn(i, 0, 0)
-                if 0 <= i - 1 < steps:
-                    normalise(i - 1, 1, 0)
-                if 0 <= i < steps:
-                    turn(i, 0, 1)
-                if 0 <= i - 1 < steps:
-                    normalise(i - 1, 1, 1)
-                if 0 <= i < steps:
-                    turn(i, 1, 0)
-                if 0 <= i - 1 < steps:
-                    store(i - 1)
+        turn_load(1, 0)
+        turn_load(1, 1)
+        scale_and_bias()
+        turn_load(1, 2)
+        linear(0)
+        regroup_weights(0, 0)
+        linear(1)
+        clamp(0)
+        exponential(0)
+        clamp(1)
+        quantise_weights(0, 0)
+        exponential(1)
+        regroup_weights(0, 1)
+        combine(0)
+        quantise_weights(0, 1)
+        turn_load(1, 3)
+        regroup_weights(1, 0)
+        turn_load(1, 4)
+        combine(1)
+        quantise(0)
+        quantise_weights(1, 0)
+        turn_load(1, 5)
+        regroup_weights(1, 1)
+        turn_load(1, 6)
+        quantise(1)
+        quantise_weights(1, 1)
+        turn_load(1, 7)
+        product(0, 0)
+        product(0, 1)
+        product(0, 2)
+        product(0, 3)
+        linear(2)
+        clamp(2)
+        exponential(2)
+        combine(2)
+        linear(3)
+        quantise(2)
+        linear(4)
+        clamp(3)
+
+        def fresh(i):
+            return range(min(passes, i + 3), min(passes, i + 4))
+
+        for i in range(steps + 1):
+            for n in fresh(i):
+                if n + 1 < passes:
+                    clamp(n + 1)
+            if i >= 1:
+                head_sums(i - 1)
+                norms(i - 1)
+                inverses(i - 1)
+            for b in range(4):
+                if i < steps:
+                    branches(i, b)
+                if i + 1 < steps:
+                    product(i + 1, b)
+            if i >= 1:
+                normalise(i - 1, 0, 0)
+                turn(i - 1, 1, 1)
+            if i < steps:
+                branch_sums(i, 0)
+                negative(i, 0)
+            if i >= 1:
+                normalise(i - 1, 0, 1)
+                normalise(i - 1, 1, 0)
+                normalise(i - 1, 1, 1)
+                store(i - 1)
+            if i < steps:
+                negative(i, 1)
+                branch_sums(i, 1)
+                turn(i, 0, 0)
+                turn(i, 0, 1)
+                turn(i, 1, 0)
+            for n in fresh(i):
+                exponential(n)
+                combine(n)
+                if n + 2 < passes:
+                    linear(n + 2)
+                quantise(n)

@@ -26,15 +26,16 @@ SHARE = P // HEADS
 ROW_TILES = ROWS // P
 K_PASS = 512
 PASSES = HID // K_PASS
-PLANES = 4 * PASSES
 
 LOAD_TILES = 4
 LOAD_COLS = LOAD_TILES * P
+LOADS = ROW_TILES // LOAD_TILES
+BN_LOADS = (1, 3)
 ROW_COLS = HID + 16
 STAT_COLS = 256
-ON_VECTOR = 1
 UNIT = 512
 STEP = 256
+ON_VECTOR = 1
 
 BN_EPS = 1e-5
 L1_EPS = 1e-12
@@ -54,7 +55,7 @@ def tile_basicemotionpredictions_pa_t_kernel(tc, h2, gamma, beta, Wh, bh, out):
     with ExitStack() as ctx:
         keep = ctx.enter_context(tc.tile_pool(name="keep", bufs=1))
         big = ctx.enter_context(tc.tile_pool(name="big", bufs=8))
-        qin = ctx.enter_context(tc.tile_pool(name="qin", bufs=3))
+        qin = ctx.enter_context(tc.tile_pool(name="qin", bufs=2))
         wraw = ctx.enter_context(tc.tile_pool(name="wraw", bufs=2))
         work = ctx.enter_context(tc.tile_pool(name="work", bufs=2))
         codes = ctx.enter_context(tc.tile_pool(name="codes", bufs=3))
@@ -64,12 +65,49 @@ def tile_basicemotionpredictions_pa_t_kernel(tc, h2, gamma, beta, Wh, bh, out):
         psum_sum = ctx.enter_context(tc.psum_pool(name="psum_sum", bufs=1))
         ctx.enter_context(tc.manual_schedule())
 
+        gamma_sb = keep.tile([P, PASSES, 4], BF16)
+        beta_sb = keep.tile([P, PASSES, 4], BF16)
+        bh_rows = keep.tile([P, P], BF16)
+        nc.vector.memset(bh_rows[:], 0.0)
+        nc.scalar.dma_start(out=gamma_sb[:], in_=gamma.rearrange("(c q t) -> q c t", c=PASSES, q=P))
+        nc.scalar.dma_start(out=beta_sb[:], in_=beta.rearrange("(c q t) -> q c t", c=PASSES, q=P))
+        nc.scalar.dma_start(
+            out=bh_rows[0:BLOCKS, :].rearrange("k (h o) -> k h o", o=SHARE),
+            in_=bh.rearrange("a g (k o) -> k (a g) o", k=BLOCKS),
+        )
+
+        loads, w_raws = [], []
+
+        def load_rows(ld):
+            x_sb = big.tile([P, LOAD_TILES, ROW_COLS], BF16, tag="big")
+            nc.vector.memset(x_sb[:, :, HID:], 1.0)
+            parts = 2 if ld == 0 else 1
+            for part in range(parts):
+                mine = slice(LOAD_TILES // parts * part, LOAD_TILES // parts * (part + 1))
+                rows = slice(LOAD_TILES * ld + mine.start, LOAD_TILES * ld + mine.stop)
+                nc.sync.dma_start(out=x_sb[:, mine, 0:HID], in_=h2_v[:, rows, :])
+            loads.append(x_sb)
+
+        def load_weights(hf):
+            w_raw = wraw.tile([P, HEADS // 2, PASSES, 4, HEAD], BF16)
+            nc.sync.dma_start(
+                out=w_raw[:].rearrange("q h c t e -> q (h c) (t e)"), in_=wh_v[:, HEADS * hf : HEADS * (hf + 1), :]
+            )
+            w_raws.append(w_raw)
+
+        for ld in range(LOADS):
+            load_rows(ld)
+            if ld in (4, 6):
+                load_weights(len(w_raws))
+
         zero = keep.tile([P, 1], F32)
         nc.vector.memset(zero[:], 0.0)
         minus_half = keep.tile([P, PASSES, 4], F32)
         nc.vector.memset(minus_half[:], -0.5)
         ln_sa = keep.tile([P, 1], F32)
         nc.vector.tensor_scalar_add(out=ln_sa[:], in0=zero[:], scalar1=math.log(SA))
+        ident = keep.tile([P, P], F32)
+        make_identity(nc, ident[:])
         neg_e0 = keep.tile([P, 1], F32)
         nc.scalar.activation(out=neg_e0[:], in_=zero[:], func=ACT.Exp, bias=ln_sa[:])
         nc.vector.tensor_scalar_mul(out=neg_e0[:], in0=neg_e0[:], scalar1=-1.0)
@@ -77,154 +115,141 @@ def tile_basicemotionpredictions_pa_t_kernel(tc, h2, gamma, beta, Wh, bh, out):
         nc.vector.tensor_scalar(
             out=exp_bias[:], in0=neg_e0[:], scalar1=-1.0 / SELU_SCALE, scalar2=math.log(SA), op0=ALU.mult, op1=ALU.add
         )
-        ident = keep.tile([P, P], F32)
-        make_identity(nc, ident[:])
-
-        gamma_sb = keep.tile([P, PASSES, 4], BF16)
-        beta_sb = keep.tile([P, PASSES, 4], BF16)
-        bh_rows = keep.tile([P, P], BF16)
-        nc.vector.memset(bh_rows[:], 0.0)
-        nc.scalar.dma_start(
-            out=bh_rows[0:BLOCKS, :].rearrange("k (h o) -> k h o", o=SHARE),
-            in_=bh.rearrange("a g (k o) -> k (a g) o", k=BLOCKS),
-        )
-        nc.scalar.dma_start(out=gamma_sb[:], in_=gamma.rearrange("(c q t) -> q c t", c=PASSES, q=P))
-        nc.scalar.dma_start(out=beta_sb[:], in_=beta.rearrange("(c q t) -> q c t", c=PASSES, q=P))
 
         x_t = keep.tile([P, PASSES, 2, ROWS], F32)
-        stats = keep.tile([P, 2, ROWS // STAT_COLS, 6], F32)
+        stats_0 = keep.tile([P, 2, LOADS, 2, 6], F32)
+        stats_1 = keep.tile([P, 2, len(BN_LOADS), 2, 6], F32)
 
         def turn_load(c, ld):
             for w in range(2):
-                xt_ps = psum_tr.tile([P, LOAD_COLS], F32, tag="tr")
+                bank = psum_tr.tile([P, LOAD_COLS], F32, tag="tr")
                 for i in range(LOAD_TILES):
                     words = loads[ld][:, i, K_PASS * c : K_PASS * (c + 1)].bitcast(F32)
-                    nc.tensor.transpose(xt_ps[:, P * i : P * (i + 1)], words[:, w::2], ident[:])
-                nc.scalar.copy(out=x_t[:, c, w, LOAD_COLS * ld : LOAD_COLS * (ld + 1)], in_=xt_ps[:])
+                    nc.tensor.transpose(bank[:, P * i : P * (i + 1)], words[:, w::2], ident[:])
+                nc.scalar.copy(out=x_t[:, c, w, LOAD_COLS * ld : LOAD_COLS * (ld + 1)], in_=bank[:])
 
-        def statistics(ld):
+        def statistics(c, ld):
+            stats, at = (stats_0, ld) if c == 0 else (stats_1, BN_LOADS.index(ld))
             for w in range(2):
                 for s in range(LOAD_COLS // STAT_COLS):
                     first = LOAD_COLS * ld + STAT_COLS * s
                     nc.vector.bn_stats(
-                        out=stats[:, w, first // STAT_COLS, :],
-                        in_=x_t[:, 0, w, first : first + STAT_COLS].bitcast(BF16),
+                        out=stats[:, w, at, s, :], in_=x_t[:, c, w, first : first + STAT_COLS].bitcast(BF16)
                     )
+
+        gram_loads = [ld for ld in range(LOADS) if ld not in BN_LOADS]
+        grams = []
 
         def gram(ld):
             for i in range(LOAD_TILES):
+                first = ld == gram_loads[0] and i == 0
+                last = ld == gram_loads[-1] and i == LOAD_TILES - 1
+                row = loads[ld][:, i, :]
                 for t in range(4):
-                    if ld == 0 and i == 0:
+                    if first:
                         bank = psum_mm.tile([P, LOAD_COLS], F32, tag="mm")
                         grams.append(bank)
-                    row = loads[ld][:, i, :]
                     nc.tensor.matmul(
                         grams[t][:, 0 : P + 1],
                         lhsT=row[:, K_PASS + t : HID : 4],
                         rhs=row[:, K_PASS + t : HID + 4 : 4],
-                        start=(ld == 0 and i == 0),
-                        stop=(ld == n_loads - 1 and i == LOAD_TILES - 1),
+                        start=first,
+                        stop=last,
                     )
 
-        loads, grams = [], []
-        n_loads = ROW_TILES // LOAD_TILES
-        for ld in range(n_loads):
-            x_sb = big.tile([P, LOAD_TILES, ROW_COLS], BF16, tag="big")
-            nc.vector.memset(x_sb[:, :, HID:], 1.0)
-            nc.sync.dma_start(out=x_sb[:, :, 0:HID], in_=h2_v[:, LOAD_TILES * ld : LOAD_TILES * (ld + 1), :])
-            loads.append(x_sb)
-        turn_load(0, 0)
-        statistics(0)
-        gram(0)
-        turn_load(0, 1)
-        statistics(1)
-        bh_f32 = keep.tile([P, P], F32)
-        nc.vector.tensor_copy(out=bh_f32[:], in_=bh_rows[:])
-        bh_ps = psum_sum.tile([P, 512], F32, tag="sum")
-        nc.tensor.transpose(bh_ps[:, 0:P], bh_f32[:], ident[:])
-        bias = keep.tile([P, OUTS // P], F32)
-        bias_exp = keep.tile([P, OUTS // P], F32)
-        nc.vector.tensor_copy(out=bias[:], in_=bh_ps[:, 0 : OUTS // P])
-        nc.vector.tensor_scalar_add(out=bias_exp[:], in0=bias[:], scalar1=math.log(SELU_ALPHA))
+        w_codes = keep.tile([P, PASSES, OUTS], U32, align_bytes=64)
+        w_scales = keep.tile([P, PASSES, OUTS], U8, align_bytes=64)
+        w_groups = []
 
-        gram(1)
-        for ld in range(2, n_loads):
-            turn_load(0, ld)
-            statistics(ld)
-            gram(ld)
+        def regroup_weights(hf, c):
+            if hf == 0:
+                w_group = work.tile([P, BLOCKS, HEADS, SHARE, 4], BF16, tag="e_exp", align_bytes=64)
+                w_groups.append(w_group)
+            for k in range(BLOCKS):
+                nc.scalar.copy(
+                    out=w_groups[c][:, k, 16 * hf : 16 * (hf + 1), :, :],
+                    in_=w_raws[hf][:, :, c, :, SHARE * k : SHARE * (k + 1)].rearrange("q h t o -> q h o t"),
+                )
 
-        w_raws = []
-        for hf in range(2):
-            w_raw = wraw.tile([P, 16, PLANES, HEAD], BF16)
-            nc.sync.dma_start(
-                out=w_raw[:].rearrange("q hg (c t) e -> q (hg c) (t e)", t=4),
-                in_=wh_v[:, 32 * hf : 32 * (hf + 1), :],
-            )
-            w_raws.append(w_raw)
+        def quantise_weights(c):
+            for half in range(2):
+                columns = slice(OUTS // 2 * half, OUTS // 2 * (half + 1))
+                nc.vector.quantize_mx(
+                    out=w_codes[:, c, columns].bitcast(FP8X4),
+                    scales=w_scales[:, c, columns],
+                    in_=w_groups[c][:, 4 * half : 4 * (half + 1)].rearrange("q k h o t -> q (k h o t)"),
+                )
 
         gamma_s = keep.tile([P, PASSES, 4], F32)
         beta_s = keep.tile([P, PASSES, 4], F32)
-        nc.vector.tensor_scalar_mul(out=gamma_s[:], in0=gamma_sb[:], scalar1=SELU_SCALE)
-        nc.vector.tensor_scalar(
-            out=beta_s[:], in0=beta_sb[:], scalar1=SELU_SCALE, scalar2=neg_e0[:], op0=ALU.mult, op1=ALU.add
-        )
+        bh_f32 = keep.tile([P, P], F32)
+        bias = keep.tile([P, BLOCKS], F32)
+        bias_exp = keep.tile([P, BLOCKS], F32)
         a_rel = keep.tile([P, PASSES, 4], F32)
         b_rel = keep.tile([P, PASSES, 4], F32)
 
+        def small_vectors():
+            nc.vector.tensor_scalar_mul(out=gamma_s[:], in0=gamma_sb[:], scalar1=SELU_SCALE)
+            nc.vector.tensor_scalar(
+                out=beta_s[:], in0=beta_sb[:], scalar1=SELU_SCALE, scalar2=neg_e0[:], op0=ALU.mult, op1=ALU.add
+            )
+            nc.vector.tensor_copy(out=bh_f32[:], in_=bh_rows[:])
+            bh_ps = psum_sum.tile([P, 512], F32, tag="sum")
+            nc.tensor.transpose(bh_ps[:, 0:P], bh_f32[:], ident[:])
+            return bh_ps
+
+        def spread_bias(bh_ps):
+            nc.vector.tensor_copy(out=bias[:], in_=bh_ps[:, 0:BLOCKS])
+            nc.vector.tensor_scalar_add(out=bias_exp[:], in0=bias[:], scalar1=math.log(SELU_ALPHA))
+
         def scale_and_bias():
+            bn_share = len(BN_LOADS) / LOADS
             mean = keep.tile([P, PASSES, 4], F32)
             var = keep.tile([P, PASSES, 4], F32)
-            mv = small.tile([P, 4, 2], F32)
-            for t in range(4):
-                nc.vector.bn_aggr(out=mv[:, t, :], in_=stats[:, t // 2, :, 3 * (t % 2) : 3 * (t % 2) + 3])
-            nc.vector.tensor_copy(out=mean[:, 0, :], in_=mv[:, :, 0])
-            nc.vector.tensor_copy(out=var[:, 0, :], in_=mv[:, :, 1])
-            square = small.tile([P, 4], F32)
+            mv = small.tile([P, PASSES, 4, 2], F32)
+            for c, stats in enumerate((stats_0, stats_1)):
+                for t in range(4):
+                    nc.vector.bn_aggr(
+                        out=mv[:, c, t, :], in_=stats[:, t // 2, :, :, 3 * (t % 2) : 3 * (t % 2) + 3].rearrange("q l s f -> q (l s) f")
+                    )
+            bn_mean = small.tile([P, 4], F32)
+            bn_square = small.tile([P, 4], F32)
+            gram_mean = small.tile([P, 4], F32)
+            gram_square = small.tile([P, 4], F32)
+            square_of_mean = small.tile([P, 4], F32)
+            nc.vector.tensor_copy(out=mean[:, 0, :], in_=mv[:, 0, :, 0])
+            nc.vector.tensor_scalar_mul(out=bn_mean[:], in0=mv[:, 1, :, 0], scalar1=bn_share)
             for t in range(4):
                 junk = small.tile([P, P], F32)
-                nc.vector.tensor_scalar_mul(out=mean[:, 1, t : t + 1], in0=grams[t][:, P : P + 1], scalar1=1.0 / ROWS)
+                nc.vector.tensor_scalar_mul(out=gram_mean[:, t : t + 1], in0=grams[t][:, P : P + 1], scalar1=1.0 / ROWS)
                 nc.vector.scalar_tensor_tensor(
                     out=junk[:], in0=grams[t][:, 0:P], scalar=1.0 / ROWS, in1=ident[:],
-                    op0=ALU.mult, op1=ALU.mult, accum_out=square[:, t : t + 1],
+                    op0=ALU.mult, op1=ALU.mult, accum_out=gram_square[:, t : t + 1],
                 )
-            square_of_mean = small.tile([P, 4], F32)
+            nc.vector.tensor_tensor(out=bn_square[:], in0=bn_mean[:], in1=mv[:, 1, :, 0], op=ALU.mult)
+            nc.vector.tensor_tensor(out=mean[:, 1, :], in0=gram_mean[:], in1=bn_mean[:], op=ALU.add)
+            nc.vector.scalar_tensor_tensor(
+                out=bn_square[:], in0=mv[:, 1, :, 1], scalar=bn_share, in1=bn_square[:], op0=ALU.mult, op1=ALU.add
+            )
             nc.vector.tensor_tensor(out=square_of_mean[:], in0=mean[:, 1, :], in1=mean[:, 1, :], op=ALU.mult)
-            nc.vector.tensor_tensor(out=var[:, 1, :], in0=square[:], in1=square_of_mean[:], op=ALU.subtract)
-            nc.vector.tensor_scalar(out=var[:], in0=var[:], scalar1=0.0, scalar2=BN_EPS, op0=ALU.max, op1=ALU.add)
+            nc.vector.tensor_tensor(out=bn_square[:], in0=gram_square[:], in1=bn_square[:], op=ALU.add)
+            nc.vector.tensor_scalar_add(out=var[:, 0, :], in0=mv[:, 0, :, 1], scalar1=BN_EPS)
+            nc.vector.tensor_tensor(out=square_of_mean[:], in0=bn_square[:], in1=square_of_mean[:], op=ALU.subtract)
+            nc.vector.tensor_scalar(
+                out=var[:, 1, :], in0=square_of_mean[:], scalar1=0.0, scalar2=BN_EPS, op0=ALU.max, op1=ALU.add
+            )
             rstd = keep.tile([P, PASSES, 4], F32)
             nc.gpsimd.tensor_tensor(out=rstd[:], in0=var[:], in1=minus_half[:], op=ALU.pow)
             nc.vector.tensor_tensor(out=a_rel[:], in0=gamma_s[:], in1=rstd[:], op=ALU.mult)
             nc.vector.tensor_tensor(out=mean[:], in0=mean[:], in1=a_rel[:], op=ALU.mult)
             nc.vector.tensor_tensor(out=b_rel[:], in0=beta_s[:], in1=mean[:], op=ALU.subtract)
 
-        w_codes = keep.tile([P, PASSES, OUTS], U32, align_bytes=64)
-        w_scales = keep.tile([P, PASSES, OUTS], U8, align_bytes=64)
-        w_groups = {}
-
-        def regroup_weights(half, c):
-            w_grouped = qin.tile([P, 4, HEADS, SHARE, 4], BF16, tag="grouped", align_bytes=64)
-            for k in range(4):
-                first = SHARE * (4 * half + k)
-                for hf in range(2):
-                    nc.vector.tensor_copy(
-                        out=w_grouped[:, k, 16 * hf : 16 * (hf + 1), :, :],
-                        in_=w_raws[hf][:, :, 4 * c : 4 * (c + 1), first : first + SHARE].rearrange("q h t o -> q h o t"),
-                    )
-            w_groups[half, c] = w_grouped
-
-        def quantise_weights(half, c):
-            nc.vector.quantize_mx(
-                out=w_codes[:, c, 512 * half : 512 * (half + 1)].bitcast(FP8X4),
-                scales=w_scales[:, c, 512 * half : 512 * (half + 1)],
-                in_=w_groups[half, c][:].rearrange("q k h o t -> q (k h o t)"),
-            )
-
         tiles = [(u, c) for u in range(ROWS // UNIT) for c in range(PASSES)]
-        e_lins, e_exps, e_groups, e_codes, e_scales = {}, {}, {}, {}, {}
+        e_lins, e_exps, e_pairs, e_groups, e_codes, e_scales = {}, {}, {}, {}, {}, {}
 
         def linear(n):
             u, c = tiles[n]
-            e_lin = work.tile([P, 4, UNIT], F32, bufs=3)
+            e_lin = work.tile([P, 4, UNIT], F32, tag="e_lin", bufs=3)
             for t in range(4):
                 words = x_t[:, c, t // 2, UNIT * u : UNIT * (u + 1)]
                 x_plane = words.bitcast(BF16).rearrange("q (j e2) -> q j e2", e2=2)[:, :, t % 2]
@@ -238,7 +263,7 @@ def tile_basicemotionpredictions_pa_t_kernel(tc, h2, gamma, beta, Wh, bh, out):
             e_lins[n] = e_lin
 
         def clamp(n):
-            e_exp = work.tile([P, 4, UNIT], F32)
+            e_exp = work.tile([P, 4, UNIT], F32, tag="e_exp", align_bytes=64)
             nc.vector.tensor_scalar(out=e_exp[:], in0=e_lins[n][:], scalar1=neg_e0[:], scalar2=None, op0=ALU.min)
             e_exps[n] = e_exp
 
@@ -246,14 +271,24 @@ def tile_basicemotionpredictions_pa_t_kernel(tc, h2, gamma, beta, Wh, bh, out):
             nc.scalar.activation(out=e_exps[n][:], in_=e_exps[n][:], func=ACT.Exp, scale=1.0 / SELU_SCALE, bias=exp_bias[:])
 
         def combine(n):
+            e_pair = work.tile([P, 2, UNIT, 2], BF16, tag="e_pair")
+            for w in range(2):
+                pair = slice(2 * w, 2 * (w + 1))
+                nc.vector.scalar_tensor_tensor(
+                    out=e_pair[:, w],
+                    in0=e_lins[n][:, pair, :].rearrange("q t j -> q j t"),
+                    scalar=neg_e0[:],
+                    in1=e_exps[n][:, pair, :].rearrange("q t j -> q j t"),
+                    op0=ALU.max,
+                    op1=ALU.add,
+                )
+            e_pairs[n] = e_pair
+
+        def interleave(n):
             e_group = qin.tile([P, UNIT, 4], BF16, tag="grouped", align_bytes=64)
-            nc.vector.scalar_tensor_tensor(
-                out=e_group[:],
-                in0=e_lins[n][:].rearrange("q t j -> q j t"),
-                scalar=neg_e0[:],
-                in1=e_exps[n][:].rearrange("q t j -> q j t"),
-                op0=ALU.max,
-                op1=ALU.add,
+            nc.vector.tensor_copy(
+                out=e_group[:].rearrange("q j t -> q (j t)").bitcast(F32).rearrange("q (j w) -> q j w", w=2),
+                in_=e_pairs[n][:].rearrange("q w j e2 -> q (w j e2)").bitcast(F32).rearrange("q (w j) -> q j w", w=2),
             )
             e_groups[n] = e_group
 
@@ -269,6 +304,8 @@ def tile_basicemotionpredictions_pa_t_kernel(tc, h2, gamma, beta, Wh, bh, out):
                 in_=e_groups[n][:].rearrange("q j t -> q (j t)"),
             )
 
+        steps = ROWS // STEP
+        passes = len(tiles)
         accs, z_exps, z_rels, sums, d_ts, r_l1s, outs = {}, {}, {}, {}, {}, {}, {}
 
         def product(i, b):
@@ -366,68 +403,97 @@ def tile_basicemotionpredictions_pa_t_kernel(tc, h2, gamma, beta, Wh, bh, out):
                 op=ALU.mult,
             )
 
-        def store(i):
-            tiles = slice(i * STEP // P, (i + 1) * STEP // P)
-            nc.sync.dma_start(out=out_v[:, tiles, :], in_=outs[i][:].rearrange("p nt h k o -> p nt (h k o)"))
+        def store(i, nt):
+            nc.sync.dma_start(
+                out=out_v[:, i * STEP // P + nt, :], in_=outs[i][:, nt].rearrange("p h k o -> p (h k o)")
+            )
 
-        passes = len(tiles)
-        steps = ROWS // STEP
-        turn_load(1, 0)
+        turn_load(0, 0)
+        statistics(0, 0)
+        gram(0)
+        turn_load(0, 1)
+        statistics(0, 1)
         turn_load(1, 1)
-        scale_and_bias()
-        turn_load(1, 2)
-        linear(0)
+        statistics(1, 1)
+        bh_ps = small_vectors()
+        turn_load(0, 2)
+        statistics(0, 2)
+        gram(2)
+        spread_bias(bh_ps)
+        turn_load(0, 3)
+        statistics(0, 3)
+        turn_load(1, 3)
+        statistics(1, 3)
+        turn_load(0, 4)
+        statistics(0, 4)
+        gram(4)
+        turn_load(0, 5)
+        statistics(0, 5)
         regroup_weights(0, 0)
+        gram(5)
+        turn_load(0, 6)
+        statistics(0, 6)
+        regroup_weights(0, 1)
+        gram(6)
+        turn_load(0, 7)
+        statistics(0, 7)
+        regroup_weights(1, 0)
+        gram(7)
+        regroup_weights(1, 1)
+        turn_load(1, 0)
+        scale_and_bias()
+        quantise_weights(0)
+        quantise_weights(1)
+        linear(0)
         linear(1)
         clamp(0)
         exponential(0)
         clamp(1)
-        quantise_weights(0, 0)
-        exponential(1)
-        regroup_weights(0, 1)
+        linear(2)
         combine(0)
-        quantise_weights(0, 1)
-        turn_load(1, 3)
-        regroup_weights(1, 0)
-        turn_load(1, 4)
+        exponential(1)
+        clamp(2)
+        interleave(0)
         combine(1)
         quantise(0)
-        quantise_weights(1, 0)
-        turn_load(1, 5)
-        regroup_weights(1, 1)
-        turn_load(1, 6)
+        exponential(2)
+        interleave(1)
+        turn_load(1, 2)
         quantise(1)
-        quantise_weights(1, 1)
-        turn_load(1, 7)
         product(0, 0)
         product(0, 1)
         product(0, 2)
         product(0, 3)
-        linear(2)
-        clamp(2)
-        exponential(2)
         combine(2)
         linear(3)
-        quantise(2)
-        linear(4)
         clamp(3)
+        linear(4)
 
         def fresh(i):
             return range(min(passes, i + 3), min(passes, i + 4))
 
         for i in range(steps + 1):
+            for n in fresh(i - 1):
+                interleave(n)
+            if i >= 1:
+                head_sums(i - 1)
+            for n in fresh(i - 1):
+                quantise(n)
+            if i >= 1:
+                norms(i - 1)
             for n in fresh(i):
                 if n + 1 < passes:
                     clamp(n + 1)
             if i >= 1:
-                head_sums(i - 1)
-                norms(i - 1)
                 inverses(i - 1)
             for b in range(4):
                 if i < steps:
                     branches(i, b)
                 if i + 1 < steps:
                     product(i + 1, b)
+            if i < 2:
+                for ld in ((4,), (5, 6, 7))[i]:
+                    turn_load(1, ld)
             if i >= 1:
                 normalise(i - 1, 0, 0)
                 turn(i - 1, 1, 1)
@@ -436,9 +502,10 @@ def tile_basicemotionpredictions_pa_t_kernel(tc, h2, gamma, beta, Wh, bh, out):
                 negative(i, 0)
             if i >= 1:
                 normalise(i - 1, 0, 1)
+                store(i - 1, 0)
                 normalise(i - 1, 1, 0)
                 normalise(i - 1, 1, 1)
-                store(i - 1)
+                store(i - 1, 1)
             if i < steps:
                 negative(i, 1)
                 branch_sums(i, 1)
@@ -450,4 +517,3 @@ def tile_basicemotionpredictions_pa_t_kernel(tc, h2, gamma, beta, Wh, bh, out):
                 combine(n)
                 if n + 2 < passes:
                     linear(n + 2)
-                quantise(n)

@@ -263,8 +263,11 @@ def tile_basicemotionpredictions_pa_t_kernel(tc, h2, gamma, beta, Wh, bh, out):
             e_lins[n] = e_lin
 
         def clamp(n):
-            e_exp = work.tile([P, 4, UNIT], F32, tag="e_exp", align_bytes=64)
-            nc.vector.tensor_scalar(out=e_exp[:], in0=e_lins[n][:], scalar1=neg_e0[:], scalar2=None, op0=ALU.min)
+            e_exp = work.tile([P, 2, UNIT, 2], F32, tag="e_exp", align_bytes=64)
+            nc.vector.tensor_scalar(
+                out=e_exp[:], in0=e_lins[n][:].rearrange("q (w t) j -> q w j t", w=2),
+                scalar1=neg_e0[:], scalar2=None, op0=ALU.min,
+            )
             e_exps[n] = e_exp
 
         def exponential(n):
@@ -278,7 +281,7 @@ def tile_basicemotionpredictions_pa_t_kernel(tc, h2, gamma, beta, Wh, bh, out):
                     out=e_pair[:, w],
                     in0=e_lins[n][:, pair, :].rearrange("q t j -> q j t"),
                     scalar=neg_e0[:],
-                    in1=e_exps[n][:, pair, :].rearrange("q t j -> q j t"),
+                    in1=e_exps[n][:, w],
                     op0=ALU.max,
                     op1=ALU.add,
                 )

import math
from contextlib import ExitStack

import concourse.bass as bass
import concourse.mybir as mybir
import concourse.tile as tile
from concourse.masks import make_identity

F32 = mybir.dt.float32
BF16 = mybir.dt.bfloat16
U32 = mybir.dt.uint32
U8 = mybir.dt.uint8
FP8X4 = mybir.dt.float8_e4m3fn_x4
ALU = mybir.AluOpType
ACT = mybir.ActivationFunctionType
AXIS = mybir.AxisListType

P = 128
ROWS = 4096
HID = 1024
OUTS = 1024
HEAD = 32
BLOCKS = OUTS // P
HEADS = OUTS // HEAD
SHARE = P // HEADS
ROW_TILES = ROWS // P
K_PASS = 512
PASSES = HID // K_PASS

LOAD_TILES = 4
LOAD_COLS = LOAD_TILES * P
LOADS = ROW_TILES // LOAD_TILES
BN_LOADS = (1, 3)
ROW_COLS = HID + 16
STAT_COLS = 256
UNIT = 512
STEP = 256
ON_VECTOR = 1

BN_EPS = 1e-5
L1_EPS = 1e-12
SELU_ALPHA = 1.6732632423543772
SELU_SCALE = 1.0507009873554805
SA = SELU_SCALE * SELU_ALPHA

FLOPS = 2 * ROWS * HID * OUTS


def tile_basicemotionpredictions_pa_t_kernel(tc, h2, gamma, beta, Wh, bh, out):
    nc = tc.nc
    h2_v = h2.rearrange("(p n) f -> p n f", n=ROW_TILES)
    out_v = out.rearrange("(p n) h g e -> p n (h g e)", n=ROW_TILES)
    wh_v = Wh.rearrange("h g (c q t) e -> q (h g c) (t e)", c=PASSES, q=P, t=4)

    with ExitStack() as ctx:
        keep = ctx.enter_context(tc.tile_pool(name="keep", bufs=1))
        big = ctx.enter_context(tc.tile_pool(name="big", bufs=8))
        qin = ctx.enter_context(tc.tile_pool(name="qin", bufs=2))
        wraw = ctx.enter_context(tc.tile_pool(name="wraw", bufs=2))
        work = ctx.enter_context(tc.tile_pool(name="work", bufs=2))
        codes = ctx.enter_context(tc.tile_pool(name="codes", bufs=3))
        small = ctx.enter_context(tc.tile_pool(name="small", bufs=3))
        psum_mm = ctx.enter_context(tc.psum_pool(name="psum_mm", bufs=4))
        psum_tr = ctx.enter_context(tc.psum_pool(name="psum_tr", bufs=3))
        psum_sum = ctx.enter_context(tc.psum_pool(name="psum_sum", bufs=1))
        ctx.enter_context(tc.manual_schedule())

        gamma_sb = keep.tile([P, PASSES, 4], BF16)
        beta_sb = keep.tile([P, PASSES, 4], BF16)
        bh_rows = keep.tile([P, P], BF16)
        nc.vector.memset(bh_rows[:], 0.0)
        nc.scalar.dma_start(out=gamma_sb[:], in_=gamma.rearrange("(c q t) -> q c t", c=PASSES, q=P))
        nc.scalar.dma_start(out=beta_sb[:], in_=beta.rearrange("(c q t) -> q c t", c=PASSES, q=P))
        nc.scalar.dma_start(
            out=bh_rows[0:BLOCKS, :].rearrange("k (h o) -> k h o", o=SHARE),
            in_=bh.rearrange("a g (k o) -> k (a g) o", k=BLOCKS),
        )

        loads, w_raws = [], []

        def load_rows(ld):
            x_sb = big.tile([P, LOAD_TILES, ROW_COLS], BF16, tag="big")
            nc.vector.memset(x_sb[:, :, HID:], 1.0)
            parts = 2 if ld == 0 else 1
            for part in range(parts):
                mine = slice(LOAD_TILES // parts * part, LOAD_TILES // parts * (part + 1))
                rows = slice(LOAD_TILES * ld + mine.start, LOAD_TILES * ld + mine.stop)
                nc.sync.dma_start(out=x_sb[:, mine, 0:HID], in_=h2_v[:, rows, :])
            loads.append(x_sb)

        def load_weights(hf):
            w_raw = wraw.tile([P, HEADS // 2, PASSES, 4, HEAD], BF16)
            nc.sync.dma_start(
                out=w_raw[:].rearrange("q h c t e -> q (h c) (t e)"), in_=wh_v[:, HEADS * hf : HEADS * (hf + 1), :]
            )
            w_raws.append(w_raw)

        for ld in range(LOADS):
            load_rows(ld)
            if ld in (4, 6):
                load_weights(len(w_raws))

        zero = keep.tile([P, 1], F32)
        nc.vector.memset(zero[:], 0.0)
        minus_half = keep.tile([P, PASSES, 4], F32)
        nc.vector.memset(minus_half[:], -0.5)
        ln_sa = keep.tile([P, 1], F32)
        nc.vector.tensor_scalar_add(out=ln_sa[:], in0=zero[:], scalar1=math.log(SA))
        ident = keep.tile([P, P], F32)
        make_identity(nc, ident[:])
        neg_e0 = keep.tile([P, 1], F32)
        nc.scalar.activation(out=neg_e0[:], in_=zero[:], func=ACT.Exp, bias=ln_sa[:])
        nc.vector.tensor_scalar_mul(out=neg_e0[:], in0=neg_e0[:], scalar1=-1.0)
        exp_bias = keep.tile([P, 1], F32)
        nc.vector.tensor_scalar(
            out=exp_bias[:], in0=neg_e0[:], scalar1=-1.0 / SELU_SCALE, scalar2=math.log(SA), op0=ALU.mult, op1=ALU.add
        )

        x_t = keep.tile([P, PASSES, 2, ROWS], F32)
        stats_0 = keep.tile([P, 2, LOADS, 2, 6], F32)
        stats_1 = keep.tile([P, 2, len(BN_LOADS), 2, 6], F32)

        def turn_load(c, ld):
            for w in range(2):
                bank = psum_tr.tile([P, LOAD_COLS], F32, tag="tr")
                for i in range(LOAD_TILES):
                    words = loads[ld][:, i, K_PASS * c : K_PASS * (c + 1)].bitcast(F32)
                    nc.tensor.transpose(bank[:, P * i : P * (i + 1)], words[:, w::2], ident[:])
                nc.scalar.copy(out=x_t[:, c, w, LOAD_COLS * ld : LOAD_COLS * (ld + 1)], in_=bank[:])

        def statistics(c, ld):
            stats, at = (stats_0, ld) if c == 0 else (stats_1, BN_LOADS.index(ld))
            for w in range(2):
                for s in range(LOAD_COLS // STAT_COLS):
                    first = LOAD_COLS * ld + STAT_COLS * s
                    nc.vector.bn_stats(
                        out=stats[:, w, at, s, :], in_=x_t[:, c, w, first : first + STAT_COLS].bitcast(BF16)
                    )

        gram_loads = [ld for ld in range(LOADS) if ld not in BN_LOADS]
        grams = []

        def gram(ld):
            for i in range(LOAD_TILES):
                first = ld == gram_loads[0] and i == 0
                last = ld == gram_loads[-1] and i == LOAD_TILES - 1
                row = loads[ld][:, i, :]
                for t in range(4):
                    if first:
                        bank = psum_mm.tile([P, LOAD_COLS], F32, tag="mm")
                        grams.append(bank)
                    nc.tensor.matmul(
                        grams[t][:, 0 : P + 1],
                        lhsT=row[:, K_PASS + t : HID : 4],
                        rhs=row[:, K_PASS + t : HID + 4 : 4],
                        start=first,
                        stop=last,
                    )

        w_codes = keep.tile([P, PASSES, OUTS], U32, align_bytes=64)
        w_scales = keep.tile([P, PASSES, OUTS], U8, align_bytes=64)
        w_groups = []

        def regroup_weights(hf, c):
            if hf == 0:
                w_group = work.tile([P, BLOCKS, HEADS, SHARE, 4], BF16, tag="e_exp", align_bytes=64)
                w_groups.append(w_group)
            for k in range(BLOCKS):
                nc.scalar.copy(
                    out=w_groups[c][:, k, 16 * hf : 16 * (hf + 1), :, :],
                    in_=w_raws[hf][:, :, c, :, SHARE * k : SHARE * (k + 1)].rearrange("q h t o -> q h o t"),
                )

        def quantise_weights(c):
            for half in range(2):
                columns = slice(OUTS // 2 * half, OUTS // 2 * (half + 1))
                nc.vector.quantize_mx(
                    out=w_codes[:, c, columns].bitcast(FP8X4),
                    scales=w_scales[:, c, columns],
                    in_=w_groups[c][:, 4 * half : 4 * (half + 1)].rearrange("q k h o t -> q (k h o t)"),
                )

        gamma_s = keep.tile([P, PASSES, 4], F32)
        beta_s = keep.tile([P, PASSES, 4], F32)
        bh_f32 = keep.tile([P, P], F32)
        bias = keep.tile([P, BLOCKS], F32)
        bias_exp = keep.tile([P, BLOCKS], F32)
        a_rel = keep.tile([P, PASSES, 4], F32)
        b_rel = keep.tile([P, PASSES, 4], F32)

        def small_vectors():
            nc.vector.tensor_scalar_mul(out=gamma_s[:], in0=gamma_sb[:], scalar1=SELU_SCALE)
            nc.vector.tensor_scalar(
                out=beta_s[:], in0=beta_sb[:], scalar1=SELU_SCALE, scalar2=neg_e0[:], op0=ALU.mult, op1=ALU.add
            )
            nc.vector.tensor_copy(out=bh_f32[:], in_=bh_rows[:])
            bh_ps = psum_sum.tile([P, 512], F32, tag="sum")
            nc.tensor.transpose(bh_ps[:, 0:P], bh_f32[:], ident[:])
            return bh_ps

        def spread_bias(bh_ps):
            nc.vector.tensor_copy(out=bias[:], in_=bh_ps[:, 0:BLOCKS])
            nc.vector.tensor_scalar_add(out=bias_exp[:], in0=bias[:], scalar1=math.log(SELU_ALPHA))

        def scale_and_bias():
            bn_share = len(BN_LOADS) / LOADS
            mean = keep.tile([P, PASSES, 4], F32)
            var = keep.tile([P, PASSES, 4], F32)
            mv = small.tile([P, PASSES, 4, 2], F32)
            for c, stats in enumerate((stats_0, stats_1)):
                for t in range(4):
                    nc.vector.bn_aggr(
                        out=mv[:, c, t, :], in_=stats[:, t // 2, :, :, 3 * (t % 2) : 3 * (t % 2) + 3].rearrange("q l s f -> q (l s) f")
                    )
            bn_mean = small.tile([P, 4], F32)
            bn_square = small.tile([P, 4], F32)
            gram_mean = small.tile([P, 4], F32)
            gram_square = small.tile([P, 4], F32)
            square_of_mean = small.tile([P, 4], F32)
            nc.vector.tensor_copy(out=mean[:, 0, :], in_=mv[:, 0, :, 0])
            nc.vector.tensor_scalar_mul(out=bn_mean[:], in0=mv[:, 1, :, 0], scalar1=bn_share)
            for t in range(4):
                junk = small.tile([P, P], F32)
                nc.vector.tensor_scalar_mul(out=gram_mean[:, t : t + 1], in0=grams[t][:, P : P + 1], scalar1=1.0 / ROWS)
                nc.vector.scalar_tensor_tensor(
                    out=junk[:], in0=grams[t][:, 0:P], scalar=1.0 / ROWS, in1=ident[:],
                    op0=ALU.mult, op1=ALU.mult, accum_out=gram_square[:, t : t + 1],
                )
            nc.vector.tensor_tensor(out=bn_square[:], in0=bn_mean[:], in1=mv[:, 1, :, 0], op=ALU.mult)
            nc.vector.tensor_tensor(out=mean[:, 1, :], in0=gram_mean[:], in1=bn_mean[:], op=ALU.add)
            nc.vector.scalar_tensor_tensor(
                out=bn_square[:], in0=mv[:, 1, :, 1], scalar=bn_share, in1=bn_square[:], op0=ALU.mult, op1=ALU.add
            )
            nc.vector.tensor_tensor(out=square_of_mean[:], in0=mean[:, 1, :], in1=mean[:, 1, :], op=ALU.mult)
            nc.vector.tensor_tensor(out=bn_square[:], in0=gram_square[:], in1=bn_square[:], op=ALU.add)
            nc.vector.tensor_scalar_add(out=var[:, 0, :], in0=mv[:, 0, :, 1], scalar1=BN_EPS)
            nc.vector.tensor_tensor(out=square_of_mean[:], in0=bn_square[:], in1=square_of_mean[:], op=ALU.subtract)
            nc.vector.tensor_scalar(
                out=var[:, 1, :], in0=square_of_mean[:], scalar1=0.0, scalar2=BN_EPS, op0=ALU.max, op1=ALU.add
            )
            rstd = keep.tile([P, PASSES, 4], F32)
            nc.gpsimd.tensor_tensor(out=rstd[:], in0=var[:], in1=minus_half[:], op=ALU.pow)
            nc.vector.tensor_tensor(out=a_rel[:], in0=gamma_s[:], in1=rstd[:], op=ALU.mult)
            nc.vector.tensor_tensor(out=mean[:], in0=mean[:], in1=a_rel[:], op=ALU.mult)
            nc.vector.tensor_tensor(out=b_rel[:], in0=beta_s[:], in1=mean[:], op=ALU.subtract)

        tiles = [(u, c) for u in range(ROWS // UNIT) for c in range(PASSES)]
        e_lins, e_exps, e_pairs, e_groups, e_codes, e_scales = {}, {}, {}, {}, {}, {}

        def linear(n):
            u, c = tiles[n]
            e_lin = work.tile([P, 4, UNIT], F32, tag="e_lin", bufs=3)
            for t in range(4):
                words = x_t[:, c, t // 2, UNIT * u : UNIT * (u + 1)]
                x_plane = words.bitcast(BF16).rearrange("q (j e2) -> q j e2", e2=2)[:, :, t % 2]
                scale, shift = a_rel[:, c, t : t + 1], b_rel[:, c, t : t + 1]
                if t < 4 - ON_VECTOR:
                    nc.scalar.activation(out=e_lin[:, t, :], in_=x_plane, func=ACT.Identity, scale=scale, bias=shift)
                else:
                    nc.vector.tensor_scalar(
                        out=e_lin[:, t, :], in0=x_plane, scalar1=scale, scalar2=shift, op0=ALU.mult, op1=ALU.add
                    )
            e_lins[n] = e_lin

        def clamp(n):
            e_exp = work.tile([P, 2, UNIT, 2], F32, tag="e_exp", align_bytes=64)
            nc.vector.tensor_scalar(
                out=e_exp[:], in0=e_lins[n][:].rearrange("q (w t) j -> q w j t", w=2),
                scalar1=neg_e0[:], scalar2=None, op0=ALU.min,
            )
            e_exps[n] = e_exp

        def exponential(n):
            nc.scalar.activation(out=e_exps[n][:], in_=e_exps[n][:], func=ACT.Exp, scale=1.0 / SELU_SCALE, bias=exp_bias[:])

        def combine(n):
            e_pair = work.tile([P, 2, UNIT, 2], BF16, tag="e_pair")
            for w in range(2):
                pair = slice(2 * w, 2 * (w + 1))
                nc.vector.scalar_tensor_tensor(
                    out=e_pair[:, w],
                    in0=e_lins[n][:, pair, :].rearrange("q t j -> q j t"),
                    scalar=neg_e0[:],
                    in1=e_exps[n][:, w],
                    op0=ALU.max,
                    op1=ALU.add,
                )
            e_pairs[n] = e_pair

        def interleave(n):
            e_group = qin.tile([P, UNIT, 4], BF16, tag="grouped", align_bytes=64)
            nc.vector.tensor_copy(
                out=e_group[:].rearrange("q j t -> q (j t)").bitcast(F32).rearrange("q (j w) -> q j w", w=2),
                in_=e_pairs[n][:].rearrange("q w j e2 -> q (w j e2)").bitcast(F32).rearrange("q (w j) -> q j w", w=2),
            )
            e_groups[n] = e_group

        def quantise(n):
            u, c = tiles[n]
            if c == 0:
                codes_u = codes.tile([P, PASSES, UNIT], U32, align_bytes=64)
                scales_u = codes.tile([P, PASSES, UNIT], U8, align_bytes=64)
                e_codes[u], e_scales[u] = codes_u, scales_u
            nc.vector.quantize_mx(
                out=e_codes[u][:, c, :].bitcast(FP8X4),
                scales=e_scales[u][:, c, :],
                in_=e_groups[n][:].rearrange("q j t -> q (j t)"),
            )

        steps = ROWS // STEP
        passes = len(tiles)
        accs, z_exps, z_rels, sums, d_ts, r_l1s, outs = {}, {}, {}, {}, {}, {}, {}

        def product(i, b):
            u, s = divmod(i, UNIT // STEP)
            rows = slice(STEP * s, STEP * (s + 1))
            acc = psum_mm.tile([P, 2, STEP], F32, tag="mm")
            for k in range(2):
                w_cols = slice(P * (2 * b + k), P * (2 * b + k + 1))
                for c in range(PASSES):
                    nc.tensor.matmul_mx(
                        out=acc[:, k, :],
                        lhsT=w_codes[:, c, w_cols].bitcast(FP8X4),
                        lhsT_scale=w_scales[:, c, w_cols],
                        rhs=e_codes[u][:, c, rows].bitcast(FP8X4),
                        rhs_scale=e_scales[u][:, c, rows],
                        start=(c == 0),
                        stop=(c == PASSES - 1),
                    )
            accs[i, b] = acc

        def branches(i, b):
            if b == 0:
                z_exp = big.tile([P, BLOCKS, STEP], F32, tag="big")
                z_rel = big.tile([P, BLOCKS, STEP], F32, tag="big")
                z_exps[i], z_rels[i] = z_exp, z_rel
            for k in range(2):
                ob = 2 * b + k
                nc.scalar.activation(
                    out=z_exps[i][:, ob, :], in_=accs[i, b][:, k, :], func=ACT.Exp, bias=bias_exp[:, ob : ob + 1]
                )
                nc.scalar.activation(
                    out=z_rels[i][:, ob, :], in_=accs[i, b][:, k, :], func=ACT.Relu, bias=bias[:, ob : ob + 1]
                )

        def negative(i, half):
            part = z_exps[i][:, 4 * half : 4 * (half + 1), :]
            nc.vector.tensor_scalar(
                out=part, in0=part, scalar1=SELU_ALPHA, scalar2=-SELU_ALPHA, op0=ALU.min, op1=ALU.add
            )

        def turn_add(out, sources):
            for n, source in enumerate(sources):
                nc.tensor.matmul(
                    out, lhsT=source, rhs=ident[:], start=(n == 0), stop=(n == len(sources) - 1), is_transpose=True
                )

        def branch_sums(i, branch):
            if branch == 0:
                total = psum_sum.tile([P, 2, STEP // P, P], F32, tag="sum")
                sums[i] = total
            z = (z_rels if branch == 0 else z_exps)[i]
            for nt in range(STEP // P):
                turn_add(sums[i][:, branch, nt, :], [z[:, k, P * nt : P * (nt + 1)] for k in range(BLOCKS)])

        def turn(i, nt, half):
            d_t = psum_tr.tile([P, 4, P], F32, tag="tr")
            for k in range(4):
                ob = 4 * half + k
                turn_add(d_t[:, k, :], [z[i][:, ob, P * nt : P * (nt + 1)] for z in (z_rels, z_exps)])
            d_ts[i, nt, half] = d_t

        parts, l1s = {}, {}

        def head_sums(i):
            part = small.tile([P, 2, STEP // P, HEADS], F32)
            nc.vector.tensor_reduce(
                out=part[:].rearrange("p b nt h -> p (b nt h)"),
                in_=sums[i][:].rearrange("p b nt (h o) -> p (b nt h) o", o=SHARE),
                axis=AXIS.X,
                op=ALU.add,
            )
            parts[i] = part

        def norms(i):
            l1 = small.tile([P, STEP // P, HEADS], F32)
            nc.vector.scalar_tensor_tensor(
                out=l1[:], in0=parts[i][:, 0], scalar=L1_EPS / SELU_SCALE, in1=parts[i][:, 1],
                op0=ALU.max, op1=ALU.subtract,
            )
            l1s[i] = l1

        def inverses(i):
            r_l1 = small.tile([P, STEP // P, HEADS], F32)
            nc.vector.reciprocal(out=r_l1[:], in_=l1s[i][:])
            r_l1s[i] = r_l1

        def normalise(i, nt, half):
            if nt == 0 and half == 0:
                out_sb = big.tile([P, STEP // P, HEADS, BLOCKS, SHARE], F32, tag="big")
                outs[i] = out_sb
            nc.vector.tensor_tensor(
                out=outs[i][:, nt, :, 4 * half : 4 * (half + 1), :].rearrange("p h k o -> p k h o"),
                in0=d_ts[i, nt, half][:].rearrange("p k (h o) -> p k h o", o=SHARE),
                in1=r_l1s[i][:, nt, :].unsqueeze(1).unsqueeze(3).to_broadcast([P, 4, HEADS, SHARE]),
                op=ALU.mult,
            )

        def store(i, nt):
            nc.sync.dma_start(
                out=out_v[:, i * STEP // P + nt, :], in_=outs[i][:, nt].rearrange("p h k o -> p (h k o)")
            )

        turn_load(0, 0)
        statistics(0, 0)
        gram(0)
        turn_load(0, 1)
        statistics(0, 1)
        turn_load(1, 1)
        statistics(1, 1)
        bh_ps = small_vectors()
        turn_load(0, 2)
        statistics(0, 2)
        gram(2)
        spread_bias(bh_ps)
        turn_load(0, 3)
        statistics(0, 3)
        turn_load(1, 3)
        statistics(1, 3)
        turn_load(0, 4)
        statistics(0, 4)
        gram(4)
        turn_load(0, 5)
        statistics(0, 5)
        regroup_weights(0, 0)
        gram(5)
        turn_load(0, 6)
        statistics(0, 6)
        regroup_weights(0, 1)
        gram(6)
        turn_load(0, 7)
        statistics(0, 7)
        regroup_weights(1, 0)
        gram(7)
        regroup_weights(1, 1)
        turn_load(1, 0)
        scale_and_bias()
        quantise_weights(0)
        quantise_weights(1)
        linear(0)
        linear(1)
        clamp(0)
        exponential(0)
        clamp(1)
        linear(2)
        combine(0)
        exponential(1)
        clamp(2)
        interleave(0)
        combine(1)
        quantise(0)
        exponential(2)
        interleave(1)
        turn_load(1, 2)
        quantise(1)
        product(0, 0)
        product(0, 1)
        product(0, 2)
        product(0, 3)
        combine(2)
        linear(3)
        clamp(3)
        linear(4)

        def fresh(i):
            return range(min(passes, i + 3), min(passes, i + 4))

        for i in range(steps + 1):
            for n in fresh(i - 1):
                interleave(n)
            if i >= 1:
                head_sums(i - 1)
            for n in fresh(i - 1):
                quantise(n)
            if i >= 1:
                norms(i - 1)
            for n in fresh(i):
                if n + 1 < passes:
                    clamp(n + 1)
            if i >= 1:
                inverses(i - 1)
            for b in range(4):
                if i < steps:
                    branches(i, b)
                if i + 1 < steps:
                    product(i + 1, b)
            if i < 2:
                for ld in ((4,), (5, 6, 7))[i]:
                    turn_load(1, ld)
            if i >= 1:
                normalise(i - 1, 0, 0)
                turn(i - 1, 1, 1)
            if i < steps:
                branch_sums(i, 0)
                negative(i, 0)
            if i >= 1:
                normalise(i - 1, 0, 1)
                store(i - 1, 0)
                normalise(i - 1, 1, 0)
                normalise(i - 1, 1, 1)
                store(i - 1, 1)
            if i < steps:
                negative(i, 1)
                branch_sums(i, 1)
                turn(i, 0, 0)
                turn(i, 0, 1)
                turn(i, 1, 0)
            for n in fresh(i):
                exponential(n)
                combine(n)
                if n + 2 < passes:
                    linear(n + 2)
